import numpy as np
import ml_dtypes


def mxq(x, axis, fmt="e4m3"):
    dtype, down = {"e4m3": (ml_dtypes.float8_e4m3fn, 7), "e5m2": (ml_dtypes.float8_e5m2, 14)}[fmt]
    v = np.moveaxis(np.asarray(x, np.float32).astype(ml_dtypes.bfloat16).astype(np.float64), axis, -1)
    blocks = v.reshape(v.shape[:-1] + (-1, 32))
    amax = np.abs(blocks).max(-1, keepdims=True)
    byte = np.maximum(np.where(amax > 0, np.frexp(amax)[1] - 1 + 127, 0) - down, 1)
    scale = np.exp2(byte - 127.0)
    codes = (blocks / scale).astype(np.float32).astype(dtype).astype(np.float64)
    return np.moveaxis((codes * scale).reshape(v.shape), -1, axis)


WIDE = False


def mx_kscale(k):
    if not WIDE:
        return np.ones(k)
    levels = np.array([10, -10, 5, -5, 0])
    if k % 512:
        return np.exp2(np.random.permutation(np.resize(levels, k // 32))).repeat(32)
    a = np.empty((k // 512, 16))
    for p in range(k // 512):
        a[p, :8] = np.random.permutation(np.resize(levels, 8))
        for g in range(8):
            far = levels[np.abs(levels - a[p, g]) >= 10]
            a[p, g + 8] = far[np.random.randint(len(far))]
    return np.exp2(a.ravel()).repeat(32)


BF16 = ml_dtypes.bfloat16


def bf(x):
    return np.asarray(x, np.float32).astype(BF16)


def f64(x):
    return np.asarray(x).astype(np.float64)


B, T, E, V, H, C = 2, 2048, 512, 2048, 4, 512
KD = E // H
ROPE_BASE = 10000.0


def rotate_every_two(u):
    u1 = u[..., ::2]
    u2 = u[..., 1::2]
    return np.stack((-u2, u1), axis=-1).reshape(u.shape)


def theta_shift(u, sin, cos):
    return u * cos + rotate_every_two(u) * sin


def setup_inputs():
    s = mx_kscale(E)
    angle = np.arange(T)[:, None] * (1.0 / ROPE_BASE ** (np.repeat(np.arange(KD // 2), 2) * 2.0 / KD))
    return {"x": bf(np.random.standard_normal((B, T, E)) * s),
            "sin": bf(np.sin(angle)), "cos": bf(np.cos(angle)),
            "Wq": bf(np.random.standard_normal((E, E)) * 0.5 / np.sqrt(E) / s[:, None]),
            "Wk": bf(np.random.standard_normal((E, E)) * 2.0 / np.sqrt(E) / s[:, None])}


def reference(x, sin, cos, Wq, Wk):
    xq = mxq(f64(x), 2, "e4m3")
    q = (xq @ mxq(f64(Wq), 0, "e4m3")).reshape(B, T, H, KD).transpose(0, 2, 1, 3)
    k = ((xq @ mxq(f64(Wk), 0, "e4m3")) * KD ** -0.5).reshape(B, T, H, KD).transpose(0, 2, 1, 3)
    return theta_shift(q, f64(sin), f64(cos)), theta_shift(k, f64(sin), f64(cos))

@@ -1,0 +1,165 @@
+from contextlib import ExitStack
+
+import concourse.mybir as mybir
+from concourse.masks import make_identity
+
+F32 = mybir.dt.float32
+BF16 = mybir.dt.bfloat16
+U32 = mybir.dt.uint32
+U8 = mybir.dt.uint8
+FP8X4 = mybir.dt.float8_e4m3fn_x4
+MULT = mybir.AluOpType.mult
+ADD = mybir.AluOpType.add
+
+P = 128
+PACK = 4
+BATCH, SEQ, WIDTH = 2, 2048, 512
+HEADS, HEAD_DIM = 4, 128
+ROWS = 4
+GROUP = P * ROWS
+GROUPS_PER_SEQ = SEQ // GROUP
+
+FLOPS = 2 * BATCH * SEQ * WIDTH * (2 * WIDTH)
+
+
+def load_weight(nc, pools, w):
+    w_rows = pools["weights"].tile([P, PACK, WIDTH], BF16)
+    nc.sync.dma_start(
+        out=w_rows[:].rearrange("p t c -> p (t c)"),
+        in_=w.rearrange("(p t) c -> p (t c)", t=PACK),
+    )
+    return w_rows
+
+
+def quantise_weight(nc, pools, w_rows, plain_copy):
+    w_grouped = pools["weights"].tile([P, 2, WIDTH, PACK], BF16, align_bytes=64)
+    plain_copy(out=w_grouped[:, 0], in_=w_rows[:].rearrange("p t c -> p c t"))
+    turned = w_grouped[:, 1].rearrange("p (i e) t -> p i e t", e=2)
+    pairs = w_rows[:].rearrange("p t (i e) -> p i e t", e=2)
+    nc.scalar.mul(out=turned[:, :, 0, :], in_=pairs[:, :, 1, :], mul=-1.0)
+    nc.scalar.copy(out=turned[:, :, 1, :], in_=pairs[:, :, 0, :])
+    w_codes = pools["weights"].tile([P, 2, WIDTH], U32, align_bytes=64)
+    w_scales = pools["weights"].tile([P, 2, WIDTH], U8, align_bytes=64)
+    nc.vector.quantize_mx(
+        out=w_codes[:].rearrange("p v c -> p (v c)").bitcast(FP8X4),
+        scales=w_scales[:].rearrange("p v c -> p (v c)"),
+        in_=w_grouped[:].rearrange("p v c t -> p (v c t)"),
+    )
+    return w_codes, w_scales
+
+
+def quantise_positions(nc, pools, identity, x_rows):
+    x_grouped = pools["x_mx"].tile([P, GROUP, PACK], BF16, align_bytes=64)
+    grouped_words = x_grouped[:].bitcast(F32)
+    for half in range(ROWS // 2):
+        x_t = pools["psum_t"].tile([P, 2, 2, P], F32)
+        for r in range(2):
+            words = x_rows[:, 2 * half + r, :].bitcast(F32)
+            for u in range(2):
+                nc.tensor.transpose(x_t[:, r, u, :], words[:, u : 2 * P : 2], identity[:])
+        nc.scalar.copy(
+            out=grouped_words[:, 2 * half * P : 2 * (half + 1) * P, :].rearrange(
+                "p (r m) u -> p r m u", r=2
+            ),
+            in_=x_t[:].rearrange("p r u m -> p r m u"),
+        )
+    x_codes = pools["x_mx"].tile([P, GROUP], U32, align_bytes=64)
+    x_scales = pools["x_mx"].tile([P, GROUP], U8, align_bytes=64)
+    nc.vector.quantize_mx(
+        out=x_codes[:].bitcast(FP8X4),
+        scales=x_scales[:],
+        in_=x_grouped[:].rearrange("p m t -> p (m t)"),
+    )
+    return x_codes, x_scales
+
+
+def tile_multiscaleretention_pa_t_kernel(tc, x, sin, cos, Wq, Wk, out_0, out_1):
+    nc = tc.nc
+    groups = [(b, g) for b in range(BATCH) for g in range(GROUPS_PER_SEQ)]
+    with ExitStack() as stack:
+        pools = {
+            "const": stack.enter_context(tc.tile_pool(name="const", bufs=1)),
+            "weights": stack.enter_context(tc.tile_pool(name="weights", bufs=2)),
+            "x_rows": stack.enter_context(tc.tile_pool(name="x_rows", bufs=len(groups))),
+            "x_mx": stack.enter_context(tc.tile_pool(name="x_mx", bufs=2)),
+            "result": stack.enter_context(tc.tile_pool(name="result", bufs=4)),
+            "psum_t": stack.enter_context(tc.psum_pool(name="psum_t", bufs=2)),
+            "psum_mx": stack.enter_context(tc.psum_pool(name="psum_mx", bufs=3)),
+        }
+        identity = pools["const"].tile([P, P], F32)
+        make_identity(nc, identity[:])
+
+        def load_positions(b, g):
+            x_rows = pools["x_rows"].tile([P, ROWS, WIDTH], BF16)
+            nc.sync.dma_start(
+                out=x_rows[:], in_=x[b].rearrange("(g p r) c -> g p r c", p=P, r=ROWS)[g]
+            )
+            return x_rows
+
+        def load_table(table, name):
+            rows = pools["const"].tile([P, GROUPS_PER_SEQ, ROWS, HEAD_DIM], BF16, name=name)
+            nc.sync.dma_start(out=rows[:], in_=table.rearrange("(g p r) c -> p g r c", p=P, r=ROWS))
+            return rows
+
+        w_rows = {"q": load_weight(nc, pools, Wq)}
+        x_groups = [load_positions(*groups[0])]
+        tables = (load_table(cos, "cos_rows"), load_table(sin, "sin_rows"))
+        w_rows["k"] = load_weight(nc, pools, Wk)
+        for b, g in groups[1:]:
+            x_groups.append(load_positions(b, g))
+
+        factor = {"q": 1.0, "k": HEAD_DIM**-0.5}
+        outputs = {"q": out_0, "k": out_1}
+        weights = {}
+
+        def project_and_rotate(which, b, g, x_codes, x_scales, adder, rows_at_once):
+            w_codes, w_scales = weights[which]
+            out_rows = outputs[which][b].rearrange("h (g p r) c -> g p h r c", p=P, r=ROWS)[g]
+            products = [
+                pools["result"].tile([P, HEADS, ROWS, HEAD_DIM], F32, name="by_cos"),
+                pools["result"].tile([P, HEADS, ROWS, HEAD_DIM], F32, name="by_sin"),
+            ]
+            for r in range(ROWS):
+                positions = slice(r * P, (r + 1) * P)
+                for v in range(2):
+                    projected = pools["psum_mx"].tile([P, WIDTH], F32, tag="projected%d" % v)
+                    nc.tensor.matmul_mx(
+                        out=projected[:],
+                        lhsT=x_codes[:, positions].bitcast(FP8X4),
+                        lhsT_scale=x_scales[:, positions],
+                        rhs=w_codes[:, v, :].bitcast(FP8X4),
+                        rhs_scale=w_scales[:, v, :],
+                        start=True,
+                        stop=True,
+                    )
+                    nc.vector.scalar_tensor_tensor(
+                        out=products[v][:, :, r, :],
+                        in0=projected[:].rearrange("p (h c) -> p h c", h=HEADS),
+                        scalar=factor[which],
+                        in1=tables[v][:, g, r, :].unsqueeze(1).to_broadcast([P, HEADS, HEAD_DIM]),
+                        op0=MULT,
+                        op1=MULT,
+                    )
+                if (r + 1) % rows_at_once == 0:
+                    done = slice(r + 1 - rows_at_once, r + 1)
+                    adder.tensor_tensor(
+                        out=products[0][:, :, done, :],
+                        in0=products[0][:, :, done, :],
+                        in1=products[1][:, :, done, :],
+                        op=ADD,
+                    )
+                    nc.sync.dma_start(out=out_rows[:, :, done, :], in_=products[0][:, :, done, :])
+
+        weights["q"] = quantise_weight(nc, pools, w_rows["q"], nc.vector.tensor_copy)
+        x_mx = quantise_positions(nc, pools, identity, x_groups[0])
+        for n, (b, g) in enumerate(groups):
+            last = n + 1 == len(groups)
+            project_and_rotate("q", b, g, x_mx[0], x_mx[1], nc.gpsimd, ROWS)
+            if n == 0:
+                weights["k"] = quantise_weight(nc, pools, w_rows["k"], nc.scalar.copy)
+            if not last:
+                next_x_mx = quantise_positions(nc, pools, identity, x_groups[n + 1])
+                project_and_rotate("k", b, g, x_mx[0], x_mx[1], nc.gpsimd, ROWS)
+                x_mx = next_x_mx
+            else:
+                project_and_rotate("k", b, g, x_mx[0], x_mx[1], nc.vector, 1)

@@ -21,145 +21,253 @@ GROUPS_PER_SEQ = SEQ // GROUP
 
 FLOPS = 2 * BATCH * SEQ * WIDTH * (2 * WIDTH)
 
-
-def load_weight(nc, pools, w):
-    w_rows = pools["weights"].tile([P, PACK, WIDTH], BF16)
-    nc.sync.dma_start(
-        out=w_rows[:].rearrange("p t c -> p (t c)"),
-        in_=w.rearrange("(p t) c -> p (t c)", t=PACK),
-    )
-    return w_rows
-
-
-def quantise_weight(nc, pools, w_rows, plain_copy):
-    w_grouped = pools["weights"].tile([P, 2, WIDTH, PACK], BF16, align_bytes=64)
-    plain_copy(out=w_grouped[:, 0], in_=w_rows[:].rearrange("p t c -> p c t"))
-    turned = w_grouped[:, 1].rearrange("p (i e) t -> p i e t", e=2)
-    pairs = w_rows[:].rearrange("p t (i e) -> p i e t", e=2)
-    nc.scalar.mul(out=turned[:, :, 0, :], in_=pairs[:, :, 1, :], mul=-1.0)
-    nc.scalar.copy(out=turned[:, :, 1, :], in_=pairs[:, :, 0, :])
-    w_codes = pools["weights"].tile([P, 2, WIDTH], U32, align_bytes=64)
-    w_scales = pools["weights"].tile([P, 2, WIDTH], U8, align_bytes=64)
-    nc.vector.quantize_mx(
-        out=w_codes[:].rearrange("p v c -> p (v c)").bitcast(FP8X4),
-        scales=w_scales[:].rearrange("p v c -> p (v c)"),
-        in_=w_grouped[:].rearrange("p v c t -> p (v c t)"),
-    )
-    return w_codes, w_scales
-
-
-def quantise_positions(nc, pools, identity, x_rows):
-    x_grouped = pools["x_mx"].tile([P, GROUP, PACK], BF16, align_bytes=64)
-    grouped_words = x_grouped[:].bitcast(F32)
-    for half in range(ROWS // 2):
-        x_t = pools["psum_t"].tile([P, 2, 2, P], F32)
-        for r in range(2):
-            words = x_rows[:, 2 * half + r, :].bitcast(F32)
-            for u in range(2):
-                nc.tensor.transpose(x_t[:, r, u, :], words[:, u : 2 * P : 2], identity[:])
-        nc.scalar.copy(
-            out=grouped_words[:, 2 * half * P : 2 * (half + 1) * P, :].rearrange(
-                "p (r m) u -> p r m u", r=2
-            ),
-            in_=x_t[:].rearrange("p r u m -> p r m u"),
-        )
-    x_codes = pools["x_mx"].tile([P, GROUP], U32, align_bytes=64)
-    x_scales = pools["x_mx"].tile([P, GROUP], U8, align_bytes=64)
-    nc.vector.quantize_mx(
-        out=x_codes[:].bitcast(FP8X4),
-        scales=x_scales[:],
-        in_=x_grouped[:].rearrange("p m t -> p (m t)"),
-    )
-    return x_codes, x_scales
+PATTERN = "NNTTNNTT" + "DTNTNTNN" * 7
+LEAD, STEP = 2, 1
+LAG = {"N": 2, "T": 2, "D": 5}
+XA, XB, XQ = 0, 2, 4
 
 
 def tile_multiscaleretention_pa_t_kernel(tc, x, sin, cos, Wq, Wk, out_0, out_1):
     nc = tc.nc
-    groups = [(b, g) for b in range(BATCH) for g in range(GROUPS_PER_SEQ)]
+    groups = [(b, g) for g in range(GROUPS_PER_SEQ) for b in range(BATCH)]
     with ExitStack() as stack:
-        pools = {
-            "const": stack.enter_context(tc.tile_pool(name="const", bufs=1)),
-            "weights": stack.enter_context(tc.tile_pool(name="weights", bufs=2)),
-            "x_rows": stack.enter_context(tc.tile_pool(name="x_rows", bufs=len(groups))),
-            "x_mx": stack.enter_context(tc.tile_pool(name="x_mx", bufs=2)),
-            "result": stack.enter_context(tc.tile_pool(name="result", bufs=4)),
-            "psum_t": stack.enter_context(tc.psum_pool(name="psum_t", bufs=2)),
-            "psum_mx": stack.enter_context(tc.psum_pool(name="psum_mx", bufs=3)),
-        }
-        identity = pools["const"].tile([P, P], F32)
-        make_identity(nc, identity[:])
+        stack.enter_context(tc.manual_schedule())
+        const = stack.enter_context(tc.tile_pool(name="const", bufs=1))
+        weights = stack.enter_context(tc.tile_pool(name="weights", bufs=2))
+        x_pool = stack.enter_context(tc.tile_pool(name="x_rows", bufs=len(groups)))
+        x_mx = stack.enter_context(tc.tile_pool(name="x_mx", bufs=3))
+        work = stack.enter_context(tc.tile_pool(name="work", bufs=6))
+        results = stack.enter_context(tc.tile_pool(name="results", bufs=8))
+        psum_x = stack.enter_context(tc.psum_pool(name="psum_x", bufs=1))
+        psum_u = stack.enter_context(tc.psum_pool(name="psum_u", bufs=5))
+        psum_o = stack.enter_context(tc.psum_pool(name="psum_o", bufs=2))
 
-        def load_positions(b, g):
-            x_rows = pools["x_rows"].tile([P, ROWS, WIDTH], BF16)
-            nc.sync.dma_start(
-                out=x_rows[:], in_=x[b].rearrange("(g p r) c -> g p r c", p=P, r=ROWS)[g]
-            )
-            return x_rows
-
-        def load_table(table, name):
-            rows = pools["const"].tile([P, GROUPS_PER_SEQ, ROWS, HEAD_DIM], BF16, name=name)
-            nc.sync.dma_start(out=rows[:], in_=table.rearrange("(g p r) c -> p g r c", p=P, r=ROWS))
+        def load_weight(w, name):
+            rows = const.tile([P, PACK, WIDTH], BF16, name=name)
+            nc.sync.dma_start(out=rows[:].rearrange("p t c -> p (t c)"), in_=w.rearrange("(p t) c -> p (t c)", t=PACK))
             return rows
 
-        w_rows = {"q": load_weight(nc, pools, Wq)}
-        x_groups = [load_positions(*groups[0])]
-        tables = (load_table(cos, "cos_rows"), load_table(sin, "sin_rows"))
-        w_rows["k"] = load_weight(nc, pools, Wk)
-        for b, g in groups[1:]:
-            x_groups.append(load_positions(b, g))
+        def load_x(b, g):
+            x_rows = x_pool.tile([P, ROWS, WIDTH], BF16)
+            nc.sync.dma_start(out=x_rows[:], in_=x[b].rearrange("(g p r) c -> g p r c", p=P, r=ROWS)[g])
+            return x_rows
+
+        cos_rows = const.tile([P, GROUPS_PER_SEQ, GROUP], BF16, name="cos_rows")
+        sin_rows = const.tile([P, GROUPS_PER_SEQ, GROUP], BF16, name="sin_rows")
+        sin_turned = const.tile([P, GROUPS_PER_SEQ, GROUP], BF16, name="sin_turned")
+
+        def load_table(table, rows, g0, g1):
+            nc.sync.dma_start(
+                out=rows[:, g0:g1, :],
+                in_=table.rearrange("(g p r) c -> p g (r c)", p=P, r=ROWS)[:, g0:g1, :],
+            )
+
+        w_rows = {"q": load_weight(Wq, "wq_rows")}
+        x_groups = [load_x(*groups[0])]
+        load_table(cos, cos_rows, 0, 1)
+        load_table(sin, sin_rows, 0, 1)
+        w_rows["k"] = load_weight(Wk, "wk_rows")
+        x_groups.append(load_x(*groups[1]))
+        load_table(cos, cos_rows, 1, GROUPS_PER_SEQ)
+        load_table(sin, sin_rows, 1, GROUPS_PER_SEQ)
+        for b, g in groups[2:]:
+            x_groups.append(load_x(b, g))
+
+        identity = const.tile([P, P], F32, name="identity")
+        make_identity(nc, identity[:])
+        swap = const.tile([P, P], F32, name="swap")
+        identity_pairs = identity[:].rearrange("p (n e) -> p n e", e=2)
+        swap_pairs = swap[:].rearrange("p (n e) -> p n e", e=2)
+        for e in range(2):
+            nc.gpsimd.tensor_copy(out=swap_pairs[:, :, e], in_=identity_pairs[:, :, 1 - e])
+        identity_bf = const.tile([P, P], BF16, name="identity_bf")
+        nc.gpsimd.tensor_copy(out=identity_bf[:], in_=identity[:])
+
+        def prepare_sin(g):
+            pairs = sin_rows[:, g, :].rearrange("p (n e) -> p n e", e=2)
+            turned = sin_turned[:, g, :].rearrange("p (n e) -> p n e", e=2)
+            nc.scalar.copy(out=turned[:, :, 0], in_=pairs[:, :, 1])
+            nc.scalar.mul(out=turned[:, :, 1], in_=pairs[:, :, 0], mul=-1.0)
+            nc.scalar.mul(out=pairs[:, :, 0], in_=pairs[:, :, 0], mul=-1.0)
+
+        tables_t = const.tile([P, GROUPS_PER_SEQ, 2, GROUP], BF16, name="tables_t")
+
+        def transpose_tables(g):
+            bank = psum_o.tile([P, 2, ROWS, P], BF16, tag="o")
+            for v, rows in enumerate((cos_rows, sin_turned)):
+                for r in range(ROWS):
+                    nc.tensor.transpose(bank[:, v, r, :], rows[:, g, r * P : (r + 1) * P], identity_bf[:])
+            nc.scalar.copy(out=tables_t[:, g, :, :].rearrange("p v n -> p (v n)"), in_=bank[:].rearrange("p v r m -> p (v r m)"))
+
+        w_mx = {}
+
+        w_laid = {}
+
+        def lay_out_weight(which, copies):
+            w_grouped = weights.tile([P, WIDTH, PACK], BF16, align_bytes=64)
+            cols = WIDTH // len(copies)
+            for i, copy in enumerate(copies):
+                part = slice(i * cols, (i + 1) * cols)
+                copy(out=w_grouped[:, part, :], in_=w_rows[which][:, :, part].rearrange("p t c -> p c t"))
+            w_laid[which] = w_grouped
+
+        def quantise_weight(which):
+            w_grouped = w_laid[which]
+            w_codes = const.tile([P, WIDTH], U32, align_bytes=64, name="w_codes_" + which)
+            w_scales = const.tile([P, WIDTH], U8, align_bytes=64, name="w_scales_" + which)
+            nc.vector.quantize_mx(
+                out=w_codes[:].bitcast(FP8X4), scales=w_scales[:], in_=w_grouped[:].rearrange("p c t -> p (c t)")
+            )
+            w_mx[which] = (w_codes, w_scales)
+
+        x_laid = {}
+
+        def transpose_x(n, halves, copies):
+            if n not in x_laid:
+                x_grouped = x_mx.tile([P, GROUP, PACK], BF16, align_bytes=64)
+                x_laid[n] = x_grouped
+            grouped_words = x_laid[n][:].bitcast(F32)
+            for half in halves:
+                x_t = psum_x.tile([P, 2, 2, P], F32)
+                for r in range(2):
+                    words = x_groups[n][:, 2 * half + r, :].bitcast(F32)
+                    for u in range(2):
+                        nc.tensor.transpose(x_t[:, r, u, :], words[:, u : 2 * P : 2], identity[:])
+                copies[half](
+                    out=grouped_words[:, 2 * half * P : 2 * (half + 1) * P, :].rearrange("p (r m) u -> p r m u", r=2),
+                    in_=x_t[:].rearrange("p r u m -> p r m u"),
+                )
+
+        def quantise_x(n):
+            x_grouped = x_laid.pop(n)
+            x_codes = x_mx.tile([P, GROUP], U32, align_bytes=64)
+            x_scales = x_mx.tile([P, GROUP], U8, align_bytes=64)
+            nc.vector.quantize_mx(
+                out=x_codes[:].bitcast(FP8X4), scales=x_scales[:], in_=x_grouped[:].rearrange("p m t -> p (m t)")
+            )
+            return x_codes, x_scales
 
         factor = {"q": 1.0, "k": HEAD_DIM**-0.5}
         outputs = {"q": out_0, "k": out_1}
-        weights = {}
 
-        def project_and_rotate(which, b, g, x_codes, x_scales, adder, rows_at_once):
-            w_codes, w_scales = weights[which]
-            out_rows = outputs[which][b].rearrange("h (g p r) c -> g p h r c", p=P, r=ROWS)[g]
-            products = [
-                pools["result"].tile([P, HEADS, ROWS, HEAD_DIM], F32, name="by_cos"),
-                pools["result"].tile([P, HEADS, ROWS, HEAD_DIM], F32, name="by_sin"),
-            ]
-            for r in range(ROWS):
-                positions = slice(r * P, (r + 1) * P)
-                for v in range(2):
-                    projected = pools["psum_mx"].tile([P, WIDTH], F32, tag="projected%d" % v)
+        units = []
+        for n, (b, g) in enumerate(groups):
+            for which in ("q", "k"):
+                for h in range(HEADS):
+                    units.append((PATTERN[len(units)], n, b, g, which, h))
+        x_ops = {}
+        banks = {}
+        products = {}
+
+        def multiply(i):
+            kind, n, b, g, which, h = units[i]
+            w_codes, w_scales = w_mx[which]
+            x_codes, x_scales = x_ops[n]
+            cols = slice(h * HEAD_DIM, (h + 1) * HEAD_DIM)
+            bank = psum_u.tile([P, GROUP], F32, tag="u")
+            banks[i] = bank
+            if kind == "N":
+                for r in range(ROWS):
+                    part = slice(r * P, (r + 1) * P)
                     nc.tensor.matmul_mx(
-                        out=projected[:],
-                        lhsT=x_codes[:, positions].bitcast(FP8X4),
-                        lhsT_scale=x_scales[:, positions],
-                        rhs=w_codes[:, v, :].bitcast(FP8X4),
-                        rhs_scale=w_scales[:, v, :],
+                        out=bank[:, part],
+                        lhsT=x_codes[:, part].bitcast(FP8X4),
+                        lhsT_scale=x_scales[:, part],
+                        rhs=w_codes[:, cols].bitcast(FP8X4),
+                        rhs_scale=w_scales[:, cols],
                         start=True,
                         stop=True,
                     )
-                    nc.vector.scalar_tensor_tensor(
-                        out=products[v][:, :, r, :],
-                        in0=projected[:].rearrange("p (h c) -> p h c", h=HEADS),
-                        scalar=factor[which],
-                        in1=tables[v][:, g, r, :].unsqueeze(1).to_broadcast([P, HEADS, HEAD_DIM]),
-                        op0=MULT,
-                        op1=MULT,
-                    )
-                if (r + 1) % rows_at_once == 0:
-                    done = slice(r + 1 - rows_at_once, r + 1)
-                    adder.tensor_tensor(
-                        out=products[0][:, :, done, :],
-                        in0=products[0][:, :, done, :],
-                        in1=products[1][:, :, done, :],
-                        op=ADD,
-                    )
-                    nc.sync.dma_start(out=out_rows[:, :, done, :], in_=products[0][:, :, done, :])
-
-        weights["q"] = quantise_weight(nc, pools, w_rows["q"], nc.vector.tensor_copy)
-        x_mx = quantise_positions(nc, pools, identity, x_groups[0])
-        for n, (b, g) in enumerate(groups):
-            last = n + 1 == len(groups)
-            project_and_rotate("q", b, g, x_mx[0], x_mx[1], nc.gpsimd, ROWS)
-            if n == 0:
-                weights["k"] = quantise_weight(nc, pools, w_rows["k"], nc.scalar.copy)
-            if not last:
-                next_x_mx = quantise_positions(nc, pools, identity, x_groups[n + 1])
-                project_and_rotate("k", b, g, x_mx[0], x_mx[1], nc.gpsimd, ROWS)
-                x_mx = next_x_mx
             else:
-                project_and_rotate("k", b, g, x_mx[0], x_mx[1], nc.vector, 1)
+                nc.tensor.matmul_mx(
+                    out=bank[:],
+                    lhsT=w_codes[:, cols].bitcast(FP8X4),
+                    lhsT_scale=w_scales[:, cols],
+                    rhs=x_codes[:].bitcast(FP8X4),
+                    rhs_scale=x_scales[:],
+                    start=True,
+                    stop=True,
+                )
+
+        def rotate(i):
+            kind, n, b, g, which, h = units[i]
+            bank = banks.pop(i)
+            prod = work.tile([P, 2, GROUP], F32, tag="prod")
+            products[i] = prod
+            if kind == "N":
+                nc.vector.scalar_tensor_tensor(
+                    out=prod[:, 0, :], in0=bank[:], scalar=factor[which], in1=cos_rows[:, g, :], op0=MULT, op1=MULT
+                )
+                nc.vector.scalar_tensor_tensor(
+                    out=prod[:, 1, :].rearrange("p (n e) -> p n e", e=2),
+                    in0=bank[:].rearrange("p (n e) -> p n e", e=2)[:, :, ::-1],
+                    scalar=factor[which],
+                    in1=sin_rows[:, g, :].rearrange("p (n e) -> p n e", e=2),
+                    op0=MULT,
+                    op1=MULT,
+                )
+            elif kind == "T":
+                nc.vector.tensor_tensor(
+                    out=prod[:], in0=bank[:].unsqueeze(1).to_broadcast([P, 2, GROUP]), in1=tables_t[:, g, :, :], op=MULT
+                )
+            else:
+                u = work.tile([P, GROUP], F32, tag="u_sb")
+                nc.scalar.copy(out=u[:], in_=bank[:])
+                nc.gpsimd.tensor_tensor(
+                    out=prod[:], in0=u[:].unsqueeze(1).to_broadcast([P, 2, GROUP]), in1=tables_t[:, g, :, :], op=MULT
+                )
+
+        def finish(i):
+            kind, n, b, g, which, h = units[i]
+            prod = products.pop(i)
+            result = results.tile([P, GROUP], F32, tag="result")
+            if kind == "N":
+                nc.gpsimd.tensor_tensor(out=result[:], in0=prod[:, 0, :], in1=prod[:, 1, :], op=ADD)
+            else:
+                bank = psum_o.tile([P, ROWS, P], F32, tag="o")
+                for r in range(ROWS):
+                    part = slice(r * P, (r + 1) * P)
+                    nc.tensor.matmul(bank[:, r, :], prod[:, 0, part], identity[:], start=True, stop=False, is_transpose=True)
+                    nc.tensor.matmul(bank[:, r, :], prod[:, 1, part], swap[:], start=False, stop=True, is_transpose=True)
+                nc.scalar.mul(out=result[:], in_=bank[:].rearrange("p r c -> p (r c)"), mul=factor[which])
+            nc.sync.dma_start(
+                out=outputs[which][b, h].rearrange("(g p r) c -> g p (r c)", p=P, r=ROWS)[g], in_=result[:]
+            )
+
+        lay_out_weight("q", (nc.vector.tensor_copy, nc.scalar.copy))
+        quantise_weight("q")
+        transpose_x(0, (0, 1), (nc.scalar.copy, nc.vector.tensor_copy))
+        x_ops[0] = quantise_x(0)
+        prepare_sin(0)
+        for i in range(LEAD):
+            multiply(i)
+        transpose_tables(0)
+        lay_out_weight("k", (nc.scalar.copy,))
+        total = len(units)
+        per_group = 2 * HEADS
+        due = {}
+        for i in range(total + max(LAG.values()) + 2):
+            n, phase = divmod(i, per_group)
+            if i == per_group // 2 - LEAD - 1:
+                quantise_weight("k")
+            if i % STEP == 0:
+                for m in range(i + LEAD, min(i + LEAD + STEP, total)):
+                    multiply(m)
+                for m in range(i, i + STEP):
+                    for f in due.pop(m, []):
+                        finish(f)
+            if i < total:
+                rotate(i)
+                due.setdefault(i + LAG[units[i][0]], []).append(i)
+            if n + 1 < len(groups):
+                next_table = n % BATCH == 0 and n // BATCH + 1 < GROUPS_PER_SEQ
+                if phase == XA:
+                    transpose_x(n + 1, (0,), (nc.scalar.copy, nc.scalar.copy))
+                if phase == XB:
+                    transpose_x(n + 1, (1,), (nc.scalar.copy, nc.scalar.copy))
+                if phase == XQ:
+                    x_ops[n + 1] = quantise_x(n + 1)
+                if phase == 2 and next_table:
+                    prepare_sin(n // BATCH + 1)
+                if phase == 5 and next_table:
+                    transpose_tables(n // BATCH + 1)

@@ -21,8 +21,8 @@ GROUPS_PER_SEQ = SEQ // GROUP
 
 FLOPS = 2 * BATCH * SEQ * WIDTH * (2 * WIDTH)
 
-PATTERN = "NNTTNNTT" + "DTNTNTNN" * 7
-LEAD, STEP = 2, 1
+PATTERN = "NNNNTNTN" + "DTNTNTNN" * 7
+LEAD, WARM = 2, 192
 LAG = {"N": 2, "T": 2, "D": 5}
 XA, XB, XQ = 0, 2, 4
 
@@ -33,11 +33,11 @@ def tile_multiscaleretention_pa_t_kernel(tc, x, sin, cos, Wq, Wk, out_0, out_1):
     with ExitStack() as stack:
         stack.enter_context(tc.manual_schedule())
         const = stack.enter_context(tc.tile_pool(name="const", bufs=1))
-        weights = stack.enter_context(tc.tile_pool(name="weights", bufs=2))
+        weights = stack.enter_context(tc.tile_pool(name="weights", bufs=4))
         x_pool = stack.enter_context(tc.tile_pool(name="x_rows", bufs=len(groups)))
         x_mx = stack.enter_context(tc.tile_pool(name="x_mx", bufs=3))
-        work = stack.enter_context(tc.tile_pool(name="work", bufs=6))
-        results = stack.enter_context(tc.tile_pool(name="results", bufs=8))
+        work = stack.enter_context(tc.tile_pool(name="work", bufs=8))
+        results = stack.enter_context(tc.tile_pool(name="results", bufs=10))
         psum_x = stack.enter_context(tc.psum_pool(name="psum_x", bufs=1))
         psum_u = stack.enter_context(tc.psum_pool(name="psum_u", bufs=5))
         psum_o = stack.enter_context(tc.psum_pool(name="psum_o", bufs=2))
@@ -47,9 +47,13 @@ def tile_multiscaleretention_pa_t_kernel(tc, x, sin, cos, Wq, Wk, out_0, out_1):
             nc.sync.dma_start(out=rows[:].rearrange("p t c -> p (t c)"), in_=w.rearrange("(p t) c -> p (t c)", t=PACK))
             return rows
 
-        def load_x(b, g):
+        def load_x(b, g, pieces=1):
             x_rows = x_pool.tile([P, ROWS, WIDTH], BF16)
-            nc.sync.dma_start(out=x_rows[:], in_=x[b].rearrange("(g p r) c -> g p r c", p=P, r=ROWS)[g])
+            for i in range(pieces):
+                part = slice(i * ROWS // pieces, (i + 1) * ROWS // pieces)
+                nc.sync.dma_start(
+                    out=x_rows[:, part, :], in_=x[b].rearrange("(g p r) c -> g p r c", p=P, r=ROWS)[g][:, part, :]
+                )
             return x_rows
 
         cos_rows = const.tile([P, GROUPS_PER_SEQ, GROUP], BF16, name="cos_rows")
@@ -62,8 +66,8 @@ def tile_multiscaleretention_pa_t_kernel(tc, x, sin, cos, Wq, Wk, out_0, out_1):
                 in_=table.rearrange("(g p r) c -> p g (r c)", p=P, r=ROWS)[:, g0:g1, :],
             )
 
+        x_groups = [load_x(*groups[0], pieces=2)]
         w_rows = {"q": load_weight(Wq, "wq_rows")}
-        x_groups = [load_x(*groups[0])]
         load_table(cos, cos_rows, 0, 1)
         load_table(sin, sin_rows, 0, 1)
         w_rows["k"] = load_weight(Wk, "wk_rows")
@@ -83,12 +87,12 @@ def tile_multiscaleretention_pa_t_kernel(tc, x, sin, cos, Wq, Wk, out_0, out_1):
         identity_bf = const.tile([P, P], BF16, name="identity_bf")
         nc.gpsimd.tensor_copy(out=identity_bf[:], in_=identity[:])
 
-        def prepare_sin(g):
+        def prepare_sin(g, copy, mul):
             pairs = sin_rows[:, g, :].rearrange("p (n e) -> p n e", e=2)
             turned = sin_turned[:, g, :].rearrange("p (n e) -> p n e", e=2)
-            nc.scalar.copy(out=turned[:, :, 0], in_=pairs[:, :, 1])
-            nc.scalar.mul(out=turned[:, :, 1], in_=pairs[:, :, 0], mul=-1.0)
-            nc.scalar.mul(out=pairs[:, :, 0], in_=pairs[:, :, 0], mul=-1.0)
+            mul(out=turned[:, :, 1], in_=pairs[:, :, 0], mul=-1.0)
+            mul(out=pairs[:, :, 0], in_=pairs[:, :, 0], mul=-1.0)
+            copy(out=turned[:, :, 0], in_=pairs[:, :, 1])
 
         tables_t = const.tile([P, GROUPS_PER_SEQ, 2, GROUP], BF16, name="tables_t")
 
@@ -101,24 +105,25 @@ def tile_multiscaleretention_pa_t_kernel(tc, x, sin, cos, Wq, Wk, out_0, out_1):
 
         w_mx = {}
 
-        w_laid = {}
+        w_parts = {}
 
-        def lay_out_weight(which, copies):
-            w_grouped = weights.tile([P, WIDTH, PACK], BF16, align_bytes=64)
-            cols = WIDTH // len(copies)
-            for i, copy in enumerate(copies):
-                part = slice(i * cols, (i + 1) * cols)
-                copy(out=w_grouped[:, part, :], in_=w_rows[which][:, :, part].rearrange("p t c -> p c t"))
-            w_laid[which] = w_grouped
+        def lay_out_weight(which, half, copy):
+            w_grouped = weights.tile([P, WIDTH // 2, PACK], BF16, align_bytes=64, tag="w_grouped")
+            part = slice(half * WIDTH // 2, (half + 1) * WIDTH // 2)
+            copy(out=w_grouped[:], in_=w_rows[which][:, :, part].rearrange("p t c -> p c t"))
+            w_parts[which, half] = w_grouped
 
-        def quantise_weight(which):
-            w_grouped = w_laid[which]
-            w_codes = const.tile([P, WIDTH], U32, align_bytes=64, name="w_codes_" + which)
-            w_scales = const.tile([P, WIDTH], U8, align_bytes=64, name="w_scales_" + which)
+        def quantise_weight(which, half):
+            if which not in w_mx:
+                w_codes = const.tile([P, WIDTH], U32, align_bytes=64, name="w_codes_" + which)
+                w_scales = const.tile([P, WIDTH], U8, align_bytes=64, name="w_scales_" + which)
+                w_mx[which] = (w_codes, w_scales)
+            part = slice(half * WIDTH // 2, (half + 1) * WIDTH // 2)
             nc.vector.quantize_mx(
-                out=w_codes[:].bitcast(FP8X4), scales=w_scales[:], in_=w_grouped[:].rearrange("p c t -> p (c t)")
+                out=w_mx[which][0][:, part].bitcast(FP8X4),
+                scales=w_mx[which][1][:, part],
+                in_=w_parts.pop((which, half))[:].rearrange("p c t -> p (c t)"),
             )
-            w_mx[which] = (w_codes, w_scales)
 
         x_laid = {}
 
@@ -166,6 +171,8 @@ def tile_multiscaleretention_pa_t_kernel(tc, x, sin, cos, Wq, Wk, out_0, out_1):
             cols = slice(h * HEAD_DIM, (h + 1) * HEAD_DIM)
             bank = psum_u.tile([P, GROUP], F32, tag="u")
             banks[i] = bank
+            if WARM:
+                nc.tensor.matmul(bank[:, 0:WARM], identity_bf[:], cos_rows[:, 0, 0:WARM], start=True, stop=True)
             if kind == "N":
                 for r in range(ROWS):
                     part = slice(r * P, (r + 1) * P)
@@ -222,7 +229,8 @@ def tile_multiscaleretention_pa_t_kernel(tc, x, sin, cos, Wq, Wk, out_0, out_1):
             prod = products.pop(i)
             result = results.tile([P, GROUP], F32, tag="result")
             if kind == "N":
-                nc.gpsimd.tensor_tensor(out=result[:], in0=prod[:, 0, :], in1=prod[:, 1, :], op=ADD)
+                adder = nc.vector if i + 1 == len(units) else nc.gpsimd
+                adder.tensor_tensor(out=result[:], in0=prod[:, 0, :], in1=prod[:, 1, :], op=ADD)
             else:
                 bank = psum_o.tile([P, ROWS, P], F32, tag="o")
                 for r in range(ROWS):
@@ -234,28 +242,39 @@ def tile_multiscaleretention_pa_t_kernel(tc, x, sin, cos, Wq, Wk, out_0, out_1):
                 out=outputs[which][b, h].rearrange("(g p r) c -> g p (r c)", p=P, r=ROWS)[g], in_=result[:]
             )
 
-        lay_out_weight("q", (nc.vector.tensor_copy, nc.scalar.copy))
-        quantise_weight("q")
-        transpose_x(0, (0, 1), (nc.scalar.copy, nc.vector.tensor_copy))
+        def negate(out, in_, mul):
+            nc.gpsimd.tensor_scalar(out=out, in0=in_, scalar1=mul, scalar2=0.0, op0=MULT, op1=ADD)
+
+        def copy_gpsimd(out, in_):
+            nc.gpsimd.tensor_scalar(out=out, in0=in_, scalar1=1.0, scalar2=0.0, op0=MULT, op1=ADD)
+
+        transpose_x(0, (0, 1), (nc.scalar.copy, nc.scalar.copy))
+        prepare_sin(0, copy_gpsimd, negate)
+        lay_out_weight("q", 0, nc.vector.tensor_copy)
         x_ops[0] = quantise_x(0)
-        prepare_sin(0)
+        quantise_weight("q", 0)
+        lay_out_weight("q", 1, nc.scalar.copy)
         for i in range(LEAD):
             multiply(i)
-        transpose_tables(0)
-        lay_out_weight("k", (nc.scalar.copy,))
         total = len(units)
         per_group = 2 * HEADS
         due = {}
         for i in range(total + max(LAG.values()) + 2):
             n, phase = divmod(i, per_group)
-            if i == per_group // 2 - LEAD - 1:
-                quantise_weight("k")
-            if i % STEP == 0:
-                for m in range(i + LEAD, min(i + LEAD + STEP, total)):
-                    multiply(m)
-                for m in range(i, i + STEP):
-                    for f in due.pop(m, []):
-                        finish(f)
+            if i == 0:
+                quantise_weight("q", 1)
+                lay_out_weight("k", 0, nc.scalar.copy)
+            if i == 1:
+                transpose_tables(0)
+                lay_out_weight("k", 1, nc.scalar.copy)
+            if i == 2:
+                quantise_weight("k", 0)
+            if i == 4:
+                quantise_weight("k", 1)
+            for m in range(i + LEAD, min(i + LEAD + 1, total)):
+                multiply(m)
+            for f in due.pop(i, []):
+                finish(f)
             if i < total:
                 rotate(i)
                 due.setdefault(i + LAG[units[i][0]], []).append(i)
@@ -268,6 +287,6 @@ def tile_multiscaleretention_pa_t_kernel(tc, x, sin, cos, Wq, Wk, out_0, out_1):
                 if phase == XQ:
                     x_ops[n + 1] = quantise_x(n + 1)
                 if phase == 2 and next_table:
-                    prepare_sin(n // BATCH + 1)
+                    prepare_sin(n // BATCH + 1, nc.scalar.copy, nc.scalar.mul)
                 if phase == 5 and next_table:
                     transpose_tables(n // BATCH + 1)

@@ -21,10 +21,12 @@ GROUPS_PER_SEQ = SEQ // GROUP
 
 FLOPS = 2 * BATCH * SEQ * WIDTH * (2 * WIDTH)
 
-PATTERN = "NNNNTNTN" + "DTNTNTNN" * 7
-LEAD, WARM = 2, 192
-LAG = {"N": 2, "T": 2, "D": 5}
-XA, XB, XQ = 0, 2, 4
+PATTERN = "NNNNNNTN" + "DTNTNTNN" * 7
+EARLY, X1Q = 2, 3
+LEAD, WARM, HALVES, PAIRED, SPLIT = 2, 48, 0, 0, 1
+LAG = {"A": 1, "N": 2, "T": 1, "D": 6}
+XSTART, XSTRIDE = 0, 16
+XPLACES, XQ, SINP, TB = (2, 4, 6, 8), 11, 4, 10
 
 
 def tile_multiscaleretention_pa_t_kernel(tc, x, sin, cos, Wq, Wk, out_0, out_1):
@@ -35,26 +37,32 @@ def tile_multiscaleretention_pa_t_kernel(tc, x, sin, cos, Wq, Wk, out_0, out_1):
         const = stack.enter_context(tc.tile_pool(name="const", bufs=1))
         weights = stack.enter_context(tc.tile_pool(name="weights", bufs=4))
         x_pool = stack.enter_context(tc.tile_pool(name="x_rows", bufs=len(groups)))
-        x_mx = stack.enter_context(tc.tile_pool(name="x_mx", bufs=3))
-        work = stack.enter_context(tc.tile_pool(name="work", bufs=8))
-        results = stack.enter_context(tc.tile_pool(name="results", bufs=10))
+        x_mx = stack.enter_context(tc.tile_pool(name="x_mx", bufs=2))
+        work = stack.enter_context(tc.tile_pool(name="work", bufs=10))
+        results = stack.enter_context(tc.tile_pool(name="results", bufs=12))
         psum_x = stack.enter_context(tc.psum_pool(name="psum_x", bufs=1))
         psum_u = stack.enter_context(tc.psum_pool(name="psum_u", bufs=5))
         psum_o = stack.enter_context(tc.psum_pool(name="psum_o", bufs=2))
 
-        def load_weight(w, name):
-            rows = const.tile([P, PACK, WIDTH], BF16, name=name)
-            nc.sync.dma_start(out=rows[:].rearrange("p t c -> p (t c)"), in_=w.rearrange("(p t) c -> p (t c)", t=PACK))
-            return rows
+        w_rows = {}
 
-        def load_x(b, g, pieces=1):
-            x_rows = x_pool.tile([P, ROWS, WIDTH], BF16)
-            for i in range(pieces):
-                part = slice(i * ROWS // pieces, (i + 1) * ROWS // pieces)
-                nc.sync.dma_start(
-                    out=x_rows[:, part, :], in_=x[b].rearrange("(g p r) c -> g p r c", p=P, r=ROWS)[g][:, part, :]
-                )
-            return x_rows
+        def load_weight(which, w, pieces):
+            if which not in w_rows:
+                rows = const.tile([P, PACK, WIDTH], BF16, name="w_rows_" + which)
+                w_rows[which] = rows
+            for part in pieces:
+                nc.sync.dma_start(out=w_rows[which][:, :, part], in_=w.rearrange("(p t) c -> p t c", t=PACK)[:, :, part])
+
+        x_groups = {}
+
+        def load_x(n, part=slice(0, ROWS)):
+            b, g = groups[n]
+            if n not in x_groups:
+                x_rows = x_pool.tile([P, ROWS, WIDTH], BF16)
+                x_groups[n] = x_rows
+            nc.sync.dma_start(
+                out=x_groups[n][:, part, :], in_=x[b].rearrange("(g p r) c -> g p r c", p=P, r=ROWS)[g][:, part, :]
+            )
 
         cos_rows = const.tile([P, GROUPS_PER_SEQ, GROUP], BF16, name="cos_rows")
         sin_rows = const.tile([P, GROUPS_PER_SEQ, GROUP], BF16, name="sin_rows")
@@ -66,16 +74,19 @@ def tile_multiscaleretention_pa_t_kernel(tc, x, sin, cos, Wq, Wk, out_0, out_1):
                 in_=table.rearrange("(g p r) c -> p g (r c)", p=P, r=ROWS)[:, g0:g1, :],
             )
 
-        x_groups = [load_x(*groups[0], pieces=2)]
-        w_rows = {"q": load_weight(Wq, "wq_rows")}
+        halves = (slice(0, WIDTH // 2), slice(WIDTH // 2, WIDTH))
+        load_x(0, slice(0, 2))
+        load_weight("q", Wq, halves[:1])
         load_table(cos, cos_rows, 0, 1)
         load_table(sin, sin_rows, 0, 1)
-        w_rows["k"] = load_weight(Wk, "wk_rows")
-        x_groups.append(load_x(*groups[1]))
+        load_x(0, slice(2, 4))
+        load_weight("q", Wq, halves[1:])
+        load_weight("k", Wk, (slice(0, WIDTH),))
+        load_x(1)
         load_table(cos, cos_rows, 1, GROUPS_PER_SEQ)
         load_table(sin, sin_rows, 1, GROUPS_PER_SEQ)
-        for b, g in groups[2:]:
-            x_groups.append(load_x(b, g))
+        for n in range(2, len(groups)):
+            load_x(n)
 
         identity = const.tile([P, P], F32, name="identity")
         make_identity(nc, identity[:])
@@ -88,10 +99,17 @@ def tile_multiscaleretention_pa_t_kernel(tc, x, sin, cos, Wq, Wk, out_0, out_1):
         nc.gpsimd.tensor_copy(out=identity_bf[:], in_=identity[:])
 
         def prepare_sin(g, copy, mul):
+            negate_sin(g, mul)
+            turn_sin(g, copy)
+
+        def negate_sin(g, mul):
+            pairs = sin_rows[:, g, :].rearrange("p (n e) -> p n e", e=2)
+            mul(out=pairs[:, :, 0], in_=pairs[:, :, 0], mul=-1.0)
+
+        def turn_sin(g, copy):
             pairs = sin_rows[:, g, :].rearrange("p (n e) -> p n e", e=2)
             turned = sin_turned[:, g, :].rearrange("p (n e) -> p n e", e=2)
-            mul(out=turned[:, :, 1], in_=pairs[:, :, 0], mul=-1.0)
-            mul(out=pairs[:, :, 0], in_=pairs[:, :, 0], mul=-1.0)
+            copy(out=turned[:, :, 1], in_=pairs[:, :, 0])
             copy(out=turned[:, :, 0], in_=pairs[:, :, 1])
 
         tables_t = const.tile([P, GROUPS_PER_SEQ, 2, GROUP], BF16, name="tables_t")
@@ -126,31 +144,51 @@ def tile_multiscaleretention_pa_t_kernel(tc, x, sin, cos, Wq, Wk, out_0, out_1):
             )
 
         x_laid = {}
+        x_ops = {}
 
-        def transpose_x(n, halves, copies):
-            if n not in x_laid:
-                x_grouped = x_mx.tile([P, GROUP, PACK], BF16, align_bytes=64)
-                x_laid[n] = x_grouped
-            grouped_words = x_laid[n][:].bitcast(F32)
-            for half in halves:
-                x_t = psum_x.tile([P, 2, 2, P], F32)
-                for r in range(2):
-                    words = x_groups[n][:, 2 * half + r, :].bitcast(F32)
-                    for u in range(2):
-                        nc.tensor.transpose(x_t[:, r, u, :], words[:, u : 2 * P : 2], identity[:])
-                copies[half](
-                    out=grouped_words[:, 2 * half * P : 2 * (half + 1) * P, :].rearrange("p (r m) u -> p r m u", r=2),
-                    in_=x_t[:].rearrange("p r u m -> p r m u"),
-                )
+        x_split = {}
 
-        def quantise_x(n):
-            x_grouped = x_laid.pop(n)
-            x_codes = x_mx.tile([P, GROUP], U32, align_bytes=64)
-            x_scales = x_mx.tile([P, GROUP], U8, align_bytes=64)
-            nc.vector.quantize_mx(
-                out=x_codes[:].bitcast(FP8X4), scales=x_scales[:], in_=x_grouped[:].rearrange("p m t -> p (m t)")
+        def split_x(n):
+            split = x_mx.tile([P, ROWS, 2, P], F32, tag="split", bufs=3)
+            nc.scalar.copy(
+                out=split[:], in_=x_groups[n][:].bitcast(F32).rearrange("p r (m u) -> p r u m", u=2)
             )
-            return x_codes, x_scales
+            x_split[n] = split
+
+        def transpose_x(ns, slot, half):
+            if ns not in x_laid:
+                x_grouped = x_mx.tile([P, len(ns) * GROUP, PACK], BF16, align_bytes=64, tag="grouped%d" % len(ns))
+                x_laid[ns] = x_grouped
+            grouped_words = x_laid[ns][:].bitcast(F32)
+            x_t = psum_x.tile([P, 2, 2, P], F32)
+            for r in range(2):
+                if ns[slot] in x_split:
+                    words = x_split[ns[slot]][:, 2 * half + r, :, :]
+                    for u in range(2):
+                        nc.tensor.transpose(x_t[:, r, u, :], words[:, u, :], identity[:])
+                    continue
+                words = x_groups[ns[slot]][:, 2 * half + r, :].bitcast(F32)
+                for u in range(2):
+                    nc.tensor.transpose(x_t[:, r, u, :], words[:, u : 2 * P : 2], identity[:])
+            first = slot * GROUP + 2 * half * P
+            nc.scalar.copy(
+                out=grouped_words[:, first : first + 2 * P, :].rearrange("p (r m) u -> p r m u", r=2),
+                in_=x_t[:].rearrange("p r u m -> p r m u"),
+            )
+
+        def quantise_x(ns, pieces=1, piece=0):
+            if ns[0] not in x_ops:
+                x_codes = x_mx.tile([P, len(ns) * GROUP], U32, align_bytes=64, tag="codes%d" % len(ns))
+                x_scales = x_mx.tile([P, len(ns) * GROUP], U8, align_bytes=64, tag="scales%d" % len(ns))
+                for slot, n in enumerate(ns):
+                    x_ops[n] = (x_codes, x_scales, slot * GROUP)
+            width = len(ns) * GROUP // pieces
+            part = slice(piece * width, (piece + 1) * width)
+            nc.vector.quantize_mx(
+                out=x_ops[ns[0]][0][:, part].bitcast(FP8X4),
+                scales=x_ops[ns[0]][1][:, part],
+                in_=x_laid[ns][:, part, :].rearrange("p m t -> p (m t)"),
+            )
 
         factor = {"q": 1.0, "k": HEAD_DIM**-0.5}
         outputs = {"q": out_0, "k": out_1}
@@ -160,56 +198,63 @@ def tile_multiscaleretention_pa_t_kernel(tc, x, sin, cos, Wq, Wk, out_0, out_1):
             for which in ("q", "k"):
                 for h in range(HEADS):
                     units.append((PATTERN[len(units)], n, b, g, which, h))
-        x_ops = {}
         banks = {}
         products = {}
 
-        def multiply(i):
+        def multiply(i, parts=(0, 1)):
             kind, n, b, g, which, h = units[i]
+            if (which, h * 2 // HEADS) in w_parts:
+                quantise_weight(which, h * 2 // HEADS)
             w_codes, w_scales = w_mx[which]
-            x_codes, x_scales = x_ops[n]
+            x_codes, x_scales, first = x_ops[n]
             cols = slice(h * HEAD_DIM, (h + 1) * HEAD_DIM)
-            bank = psum_u.tile([P, GROUP], F32, tag="u")
-            banks[i] = bank
-            if WARM:
-                nc.tensor.matmul(bank[:, 0:WARM], identity_bf[:], cos_rows[:, 0, 0:WARM], start=True, stop=True)
-            if kind == "N":
-                for r in range(ROWS):
-                    part = slice(r * P, (r + 1) * P)
+            if i not in banks:
+                bank = psum_u.tile([P, GROUP], F32, tag="u")
+                banks[i] = bank
+            bank = banks[i]
+            for part in parts:
+                if part == 0 and WARM:
+                    nc.tensor.matmul(bank[:, 0:WARM], identity[:], identity[:, 0:WARM], start=True, stop=True)
+                if kind in "NA":
+                    for r in (2 * part, 2 * part + 1):
+                        rows = slice(first + r * P, first + (r + 1) * P)
+                        nc.tensor.matmul_mx(
+                            out=bank[:, r * P : (r + 1) * P],
+                            lhsT=x_codes[:, rows].bitcast(FP8X4),
+                            lhsT_scale=x_scales[:, rows],
+                            rhs=w_codes[:, cols].bitcast(FP8X4),
+                            rhs_scale=w_scales[:, cols],
+                            start=True,
+                            stop=True,
+                        )
+                else:
+                    rows = slice(first + part * 2 * P, first + (part + 1) * 2 * P)
                     nc.tensor.matmul_mx(
-                        out=bank[:, part],
-                        lhsT=x_codes[:, part].bitcast(FP8X4),
-                        lhsT_scale=x_scales[:, part],
-                        rhs=w_codes[:, cols].bitcast(FP8X4),
-                        rhs_scale=w_scales[:, cols],
+                        out=bank[:, part * 2 * P : (part + 1) * 2 * P],
+                        lhsT=w_codes[:, cols].bitcast(FP8X4),
+                        lhsT_scale=w_scales[:, cols],
+                        rhs=x_codes[:, rows].bitcast(FP8X4),
+                        rhs_scale=x_scales[:, rows],
                         start=True,
                         stop=True,
                     )
-            else:
-                nc.tensor.matmul_mx(
-                    out=bank[:],
-                    lhsT=w_codes[:, cols].bitcast(FP8X4),
-                    lhsT_scale=w_scales[:, cols],
-                    rhs=x_codes[:].bitcast(FP8X4),
-                    rhs_scale=x_scales[:],
-                    start=True,
-                    stop=True,
-                )
 
-        def rotate(i):
+        def rotate(i, cols=slice(0, GROUP)):
             kind, n, b, g, which, h = units[i]
-            bank = banks.pop(i)
-            prod = work.tile([P, 2, GROUP], F32, tag="prod")
-            products[i] = prod
-            if kind == "N":
+            bank = banks[i]
+            if i not in products:
+                prod = work.tile([P, 2, GROUP], F32, tag="prod")
+                products[i] = prod
+            prod = products[i]
+            if kind in "NA":
                 nc.vector.scalar_tensor_tensor(
-                    out=prod[:, 0, :], in0=bank[:], scalar=factor[which], in1=cos_rows[:, g, :], op0=MULT, op1=MULT
+                    out=prod[:, 0, cols], in0=bank[:, cols], scalar=factor[which], in1=cos_rows[:, g, cols], op0=MULT, op1=MULT
                 )
                 nc.vector.scalar_tensor_tensor(
-                    out=prod[:, 1, :].rearrange("p (n e) -> p n e", e=2),
-                    in0=bank[:].rearrange("p (n e) -> p n e", e=2)[:, :, ::-1],
+                    out=prod[:, 1, cols].rearrange("p (n e) -> p n e", e=2),
+                    in0=bank[:, cols].rearrange("p (n e) -> p n e", e=2)[:, :, ::-1],
                     scalar=factor[which],
-                    in1=sin_rows[:, g, :].rearrange("p (n e) -> p n e", e=2),
+                    in1=sin_rows[:, g, cols].rearrange("p (n e) -> p n e", e=2),
                     op0=MULT,
                     op1=MULT,
                 )
@@ -228,8 +273,8 @@ def tile_multiscaleretention_pa_t_kernel(tc, x, sin, cos, Wq, Wk, out_0, out_1):
             kind, n, b, g, which, h = units[i]
             prod = products.pop(i)
             result = results.tile([P, GROUP], F32, tag="result")
-            if kind == "N":
-                adder = nc.vector if i + 1 == len(units) else nc.gpsimd
+            if kind in "NA":
+                adder = nc.vector if i + 1 == len(units) or kind == "A" else nc.gpsimd
                 adder.tensor_tensor(out=result[:], in0=prod[:, 0, :], in1=prod[:, 1, :], op=ADD)
             else:
                 bank = psum_o.tile([P, ROWS, P], F32, tag="o")
@@ -242,51 +287,62 @@ def tile_multiscaleretention_pa_t_kernel(tc, x, sin, cos, Wq, Wk, out_0, out_1):
                 out=outputs[which][b, h].rearrange("(g p r) c -> g p (r c)", p=P, r=ROWS)[g], in_=result[:]
             )
 
-        def negate(out, in_, mul):
-            nc.gpsimd.tensor_scalar(out=out, in0=in_, scalar1=mul, scalar2=0.0, op0=MULT, op1=ADD)
-
-        def copy_gpsimd(out, in_):
-            nc.gpsimd.tensor_scalar(out=out, in0=in_, scalar1=1.0, scalar2=0.0, op0=MULT, op1=ADD)
-
-        transpose_x(0, (0, 1), (nc.scalar.copy, nc.scalar.copy))
-        prepare_sin(0, copy_gpsimd, negate)
+        early = (slice(0, GROUP // 2), slice(GROUP // 2, GROUP))
+        transpose_x((0,), 0, 0)
         lay_out_weight("q", 0, nc.vector.tensor_copy)
-        x_ops[0] = quantise_x(0)
-        quantise_weight("q", 0)
+        quantise_x((0,), 2, 0)
+        negate_sin(0, nc.scalar.mul)
+        transpose_x((0,), 0, 1)
         lay_out_weight("q", 1, nc.scalar.copy)
-        for i in range(LEAD):
+        for i in range(EARLY):
+            multiply(i, (0,))
+        for i in range(EARLY):
+            rotate(i, early[0])
+        quantise_x((0,), 2, 1)
+        for i in range(EARLY):
+            multiply(i, (1,))
+        for i in range(EARLY, LEAD):
             multiply(i)
+        lay_out_weight("k", 0, nc.scalar.copy)
+        lay_out_weight("k", 1, nc.scalar.copy)
         total = len(units)
         per_group = 2 * HEADS
         due = {}
         for i in range(total + max(LAG.values()) + 2):
             n, phase = divmod(i, per_group)
-            if i == 0:
-                quantise_weight("q", 1)
-                lay_out_weight("k", 0, nc.scalar.copy)
-            if i == 1:
-                transpose_tables(0)
-                lay_out_weight("k", 1, nc.scalar.copy)
-            if i == 2:
-                quantise_weight("k", 0)
-            if i == 4:
-                quantise_weight("k", 1)
-            for m in range(i + LEAD, min(i + LEAD + 1, total)):
-                multiply(m)
+            m = i + LEAD
+            if m < total:
+                multiply(m, (0,) if HALVES else (0, 1))
             for f in due.pop(i, []):
                 finish(f)
+            if HALVES and m < total:
+                multiply(m, (1,))
             if i < total:
-                rotate(i)
-                due.setdefault(i + LAG[units[i][0]], []).append(i)
-            if n + 1 < len(groups):
-                next_table = n % BATCH == 0 and n // BATCH + 1 < GROUPS_PER_SEQ
-                if phase == XA:
-                    transpose_x(n + 1, (0,), (nc.scalar.copy, nc.scalar.copy))
-                if phase == XB:
-                    transpose_x(n + 1, (1,), (nc.scalar.copy, nc.scalar.copy))
-                if phase == XQ:
-                    x_ops[n + 1] = quantise_x(n + 1)
-                if phase == 2 and next_table:
-                    prepare_sin(n // BATCH + 1, nc.scalar.copy, nc.scalar.mul)
-                if phase == 5 and next_table:
-                    transpose_tables(n // BATCH + 1)
+                rotate(i, early[1] if i < EARLY else slice(0, GROUP))
+                lag = LAG[units[i][0]]
+                if PAIRED and units[i][0] in "TD":
+                    lag += (i + lag) % 2
+                due.setdefault(i + lag, []).append(i)
+            if n == 0:
+                if phase in (0, 1):
+                    transpose_x((1,), 0, phase)
+                if phase == 2:
+                    turn_sin(0, nc.scalar.copy)
+                    transpose_tables(0)
+                if phase == X1Q:
+                    quantise_x((1,))
+            for pair in range(1, GROUPS_PER_SEQ):
+                ns = (BATCH * pair, BATCH * pair + 1)
+                place = i - XSTART - XSTRIDE * (pair - 1)
+                if SPLIT and place in (0, 1):
+                    split_x(ns[place])
+                if place in XPLACES:
+                    for k in range(4):
+                        if XPLACES[k] == place:
+                            transpose_x(ns, k // 2, k % 2)
+                if place == XQ:
+                    quantise_x(ns)
+                if place == SINP:
+                    prepare_sin(pair, nc.scalar.copy, nc.scalar.mul)
+                if place == TB:
+                    transpose_tables(pair)

@@ -21,12 +21,13 @@ GROUPS_PER_SEQ = SEQ // GROUP
 
 FLOPS = 2 * BATCH * SEQ * WIDTH * (2 * WIDTH)
 
-PATTERN = "NNNNNNTN" + "DTNTNTNN" * 7
-EARLY, X1Q = 2, 3
-LEAD, WARM, HALVES, PAIRED, SPLIT = 2, 48, 0, 0, 1
-LAG = {"A": 1, "N": 2, "T": 1, "D": 6}
+PATTERN = "NNNNNNTN" + "DTTNNTNN" * 7
+X1P = (1, 2)
+EARLY, X1Q, TURN, TABLES, KLAY = 2, 5, 1, 3, 1
+LEAD, STEP, WARM, PAIRED, SPLIT = 2, 2, 64, 1, 1
+LAG = {"A": 1, "N": 1, "T": 1, "D": 6}
 XSTART, XSTRIDE = 0, 16
-XPLACES, XQ, SINP, TB = (2, 4, 6, 8), 11, 4, 10
+XPLACES, XQ, SINP, TB = (3, 5, 7, 9), 12, 4, 13
 
 
 def tile_multiscaleretention_pa_t_kernel(tc, x, sin, cos, Wq, Wk, out_0, out_1):
@@ -303,31 +304,35 @@ def tile_multiscaleretention_pa_t_kernel(tc, x, sin, cos, Wq, Wk, out_0, out_1):
             multiply(i, (1,))
         for i in range(EARLY, LEAD):
             multiply(i)
-        lay_out_weight("k", 0, nc.scalar.copy)
-        lay_out_weight("k", 1, nc.scalar.copy)
+        if TURN < 0:
+            turn_sin(0, nc.scalar.copy)
+        lay_out_weight("k", 0, nc.scalar.copy if KLAY == 0 else nc.vector.tensor_copy)
+        if KLAY < 2:
+            lay_out_weight("k", 1, nc.scalar.copy)
         total = len(units)
         per_group = 2 * HEADS
         due = {}
         for i in range(total + max(LAG.values()) + 2):
             n, phase = divmod(i, per_group)
-            m = i + LEAD
-            if m < total:
-                multiply(m, (0,) if HALVES else (0, 1))
+            if i % STEP == 0:
+                for m in range(i + LEAD, min(i + LEAD + STEP, total)):
+                    multiply(m)
             for f in due.pop(i, []):
                 finish(f)
-            if HALVES and m < total:
-                multiply(m, (1,))
             if i < total:
                 rotate(i, early[1] if i < EARLY else slice(0, GROUP))
                 lag = LAG[units[i][0]]
-                if PAIRED and units[i][0] in "TD":
-                    lag += (i + lag) % 2
+                if units[i][0] in "TD":
+                    lag += -(i + lag) % PAIRED
                 due.setdefault(i + lag, []).append(i)
             if n == 0:
-                if phase in (0, 1):
-                    transpose_x((1,), 0, phase)
-                if phase == 2:
+                if phase == 1 and KLAY == 2:
+                    lay_out_weight("k", 1, nc.vector.tensor_copy)
+                if phase in X1P:
+                    transpose_x((1,), 0, X1P.index(phase))
+                if phase == TURN:
                     turn_sin(0, nc.scalar.copy)
+                if phase == TABLES:
                     transpose_tables(0)
                 if phase == X1Q:
                     quantise_x((1,))

@@ -22,9 +22,9 @@ GROUPS_PER_SEQ = SEQ // GROUP
 FLOPS = 2 * BATCH * SEQ * WIDTH * (2 * WIDTH)
 
 PATTERN = "NNNNNNTN" + "DTTNNTNN" * 7
-X1P = (1, 2)
+X1P, DEARLY = (1, 2), 0
 EARLY, X1Q, TURN, TABLES, KLAY = 2, 5, 1, 3, 1
-LEAD, STEP, WARM, PAIRED, SPLIT = 2, 2, 64, 1, 1
+LEAD, STEP, WARM, PAIRED, SPLIT = 2, 2, 160, 1, 1
 LAG = {"A": 1, "N": 1, "T": 1, "D": 6}
 XSTART, XSTRIDE = 0, 16
 XPLACES, XQ, SINP, TB = (3, 5, 7, 9), 12, 4, 13
@@ -215,7 +215,7 @@ def tile_multiscaleretention_pa_t_kernel(tc, x, sin, cos, Wq, Wk, out_0, out_1):
             bank = banks[i]
             for part in parts:
                 if part == 0 and WARM:
-                    nc.tensor.matmul(bank[:, 0:WARM], identity[:], identity[:, 0:WARM], start=True, stop=True)
+                    nc.tensor.matmul(bank[:, 0:WARM], identity_bf[:], cos_rows[:, 0, 0:WARM], start=True, stop=True)
                 if kind in "NA":
                     for r in (2 * part, 2 * part + 1):
                         rows = slice(first + r * P, first + (r + 1) * P)
@@ -317,10 +317,13 @@ def tile_multiscaleretention_pa_t_kernel(tc, x, sin, cos, Wq, Wk, out_0, out_1):
             if i % STEP == 0:
                 for m in range(i + LEAD, min(i + LEAD + STEP, total)):
                     multiply(m)
+                    if DEARLY and units[m][0] == "D":
+                        rotate(m)
             for f in due.pop(i, []):
                 finish(f)
             if i < total:
-                rotate(i, early[1] if i < EARLY else slice(0, GROUP))
+                if not (DEARLY and units[i][0] == "D"):
+                    rotate(i, early[1] if i < EARLY else slice(0, GROUP))
                 lag = LAG[units[i][0]]
                 if units[i][0] in "TD":
                     lag += -(i + lag) % PAIRED

@@ -22,10 +22,10 @@ GROUPS_PER_SEQ = SEQ // GROUP
 FLOPS = 2 * BATCH * SEQ * WIDTH * (2 * WIDTH)
 
 PATTERN = "NNNNNNTN" + "DTTNNTNN" * 7
-X1P, DEARLY = (1, 2), 0
-EARLY, X1Q, TURN, TABLES, KLAY = 2, 5, 1, 3, 1
-LEAD, STEP, WARM, PAIRED, SPLIT = 2, 2, 160, 1, 1
-LAG = {"A": 1, "N": 1, "T": 1, "D": 6}
+X1P, DEARLY, TAIL, GSPLIT = (1, 2), 0, 1, 0
+EARLY, X1Q, TURN, TABLES, QLAY, KLAY = 2, 5, 1, 3, 1, 0
+LEAD, STEP, WARM, PAIRED, SPLIT = 2, 2, 0, 1, 1
+LAG = {"A": 1, "G": 1, "N": 1, "T": 1, "D": 6}
 XSTART, XSTRIDE = 0, 16
 XPLACES, XQ, SINP, TB = (3, 5, 7, 9), 12, 4, 13
 
@@ -40,7 +40,8 @@ def tile_multiscaleretention_pa_t_kernel(tc, x, sin, cos, Wq, Wk, out_0, out_1):
         x_pool = stack.enter_context(tc.tile_pool(name="x_rows", bufs=len(groups)))
         x_mx = stack.enter_context(tc.tile_pool(name="x_mx", bufs=2))
         work = stack.enter_context(tc.tile_pool(name="work", bufs=10))
-        results = stack.enter_context(tc.tile_pool(name="results", bufs=12))
+        slow = stack.enter_context(tc.tile_pool(name="slow", bufs=3))
+        results = stack.enter_context(tc.tile_pool(name="results", bufs=10))
         psum_x = stack.enter_context(tc.psum_pool(name="psum_x", bufs=1))
         psum_u = stack.enter_context(tc.psum_pool(name="psum_u", bufs=5))
         psum_o = stack.enter_context(tc.psum_pool(name="psum_o", bufs=2))
@@ -216,7 +217,7 @@ def tile_multiscaleretention_pa_t_kernel(tc, x, sin, cos, Wq, Wk, out_0, out_1):
             for part in parts:
                 if part == 0 and WARM:
                     nc.tensor.matmul(bank[:, 0:WARM], identity_bf[:], cos_rows[:, 0, 0:WARM], start=True, stop=True)
-                if kind in "NA":
+                if kind in "NAG":
                     for r in (2 * part, 2 * part + 1):
                         rows = slice(first + r * P, first + (r + 1) * P)
                         nc.tensor.matmul_mx(
@@ -244,10 +245,22 @@ def tile_multiscaleretention_pa_t_kernel(tc, x, sin, cos, Wq, Wk, out_0, out_1):
             kind, n, b, g, which, h = units[i]
             bank = banks[i]
             if i not in products:
-                prod = work.tile([P, 2, GROUP], F32, tag="prod")
-                products[i] = prod
+                if kind in "DG":
+                    products[i] = slow.tile([P, 2, GROUP], F32, tag="prod_d", name="prod_d")
+                else:
+                    products[i] = work.tile([P, 2, GROUP], F32, tag="prod", name="prod")
             prod = products[i]
-            if kind in "NA":
+            if kind == "G":
+                u = slow.tile([P, GROUP], F32, tag="u_sb")
+                nc.scalar.mul(out=u[:, cols], in_=bank[:, cols], mul=factor[which])
+                nc.gpsimd.tensor_tensor(out=prod[:, 0, cols], in0=u[:, cols], in1=cos_rows[:, g, cols], op=MULT)
+                nc.gpsimd.tensor_tensor(
+                    out=prod[:, 1, cols].rearrange("p (n e) -> p n e", e=2),
+                    in0=u[:, cols].rearrange("p (n e) -> p n e", e=2)[:, :, ::-1],
+                    in1=sin_rows[:, g, cols].rearrange("p (n e) -> p n e", e=2),
+                    op=MULT,
+                )
+            elif kind in "NA":
                 nc.vector.scalar_tensor_tensor(
                     out=prod[:, 0, cols], in0=bank[:, cols], scalar=factor[which], in1=cos_rows[:, g, cols], op0=MULT, op1=MULT
                 )
@@ -264,7 +277,7 @@ def tile_multiscaleretention_pa_t_kernel(tc, x, sin, cos, Wq, Wk, out_0, out_1):
                     out=prod[:], in0=bank[:].unsqueeze(1).to_broadcast([P, 2, GROUP]), in1=tables_t[:, g, :, :], op=MULT
                 )
             else:
-                u = work.tile([P, GROUP], F32, tag="u_sb")
+                u = slow.tile([P, GROUP], F32, tag="u_sb")
                 nc.scalar.copy(out=u[:], in_=bank[:])
                 nc.gpsimd.tensor_tensor(
                     out=prod[:], in0=u[:].unsqueeze(1).to_broadcast([P, 2, GROUP]), in1=tables_t[:, g, :, :], op=MULT
@@ -274,9 +287,19 @@ def tile_multiscaleretention_pa_t_kernel(tc, x, sin, cos, Wq, Wk, out_0, out_1):
             kind, n, b, g, which, h = units[i]
             prod = products.pop(i)
             result = results.tile([P, GROUP], F32, tag="result")
-            if kind in "NA":
+            if kind in "NAG":
+                if i + 1 == len(units) and TAIL > 1:
+                    view = outputs[which][b, h].rearrange("(g p r) c -> g p (r c)", p=P, r=ROWS)[g]
+                    for t in range(TAIL):
+                        part = slice(t * GROUP // TAIL, (t + 1) * GROUP // TAIL)
+                        nc.vector.tensor_tensor(out=result[:, part], in0=prod[:, 0, part], in1=prod[:, 1, part], op=ADD)
+                        nc.sync.dma_start(out=view[:, part], in_=result[:, part])
+                    return
                 adder = nc.vector if i + 1 == len(units) or kind == "A" else nc.gpsimd
-                adder.tensor_tensor(out=result[:], in0=prod[:, 0, :], in1=prod[:, 1, :], op=ADD)
+                pieces = 2 if any(0 <= XQ + XSTRIDE * s - i < GSPLIT for s in range(GROUPS_PER_SEQ - 1)) else 1
+                for t in range(pieces):
+                    part = slice(t * GROUP // pieces, (t + 1) * GROUP // pieces)
+                    adder.tensor_tensor(out=result[:, part], in0=prod[:, 0, part], in1=prod[:, 1, part], op=ADD)
             else:
                 bank = psum_o.tile([P, ROWS, P], F32, tag="o")
                 for r in range(ROWS):
@@ -294,9 +317,12 @@ def tile_multiscaleretention_pa_t_kernel(tc, x, sin, cos, Wq, Wk, out_0, out_1):
         quantise_x((0,), 2, 0)
         negate_sin(0, nc.scalar.mul)
         transpose_x((0,), 0, 1)
-        lay_out_weight("q", 1, nc.scalar.copy)
+        if QLAY == 0:
+            lay_out_weight("q", 1, nc.scalar.copy)
         for i in range(EARLY):
             multiply(i, (0,))
+        if QLAY == 1:
+            lay_out_weight("q", 1, nc.vector.tensor_copy)
         for i in range(EARLY):
             rotate(i, early[0])
         quantise_x((0,), 2, 1)
@@ -322,7 +348,10 @@ def tile_multiscaleretention_pa_t_kernel(tc, x, sin, cos, Wq, Wk, out_0, out_1):
             for f in due.pop(i, []):
                 finish(f)
             if i < total:
-                if not (DEARLY and units[i][0] == "D"):
+                if i + 1 == total:
+                    for t in range(TAIL):
+                        rotate(i, slice(t * GROUP // TAIL, (t + 1) * GROUP // TAIL))
+                elif not (DEARLY and units[i][0] == "D"):
                     rotate(i, early[1] if i < EARLY else slice(0, GROUP))
                 lag = LAG[units[i][0]]
                 if units[i][0] in "TD":

@@ -21,13 +21,14 @@ GROUPS_PER_SEQ = SEQ // GROUP
 
 FLOPS = 2 * BATCH * SEQ * WIDTH * (2 * WIDTH)
 
-PATTERN = "NNNNNNTN" + "DTTNNTNN" * 7
-X1P, DEARLY, TAIL, GSPLIT = (1, 2), 0, 1, 0
+PATTERN = "NNNNNNTNDTTNTNNN" + "DTTNNTNNDTTNTNNN" * 3
+KWHOLE = 1
+X1P, DEARLY, TAIL, XROWS = (1, 2), 0, 2, 1
 EARLY, X1Q, TURN, TABLES, QLAY, KLAY = 2, 5, 1, 3, 1, 0
 LEAD, STEP, WARM, PAIRED, SPLIT = 2, 2, 0, 1, 1
 LAG = {"A": 1, "G": 1, "N": 1, "T": 1, "D": 6}
 XSTART, XSTRIDE = 0, 16
-XPLACES, XQ, SINP, TB = (3, 5, 7, 9), 12, 4, 13
+XPLACES, XQ, SINP, TB = (4, 6, 8, 10), 13, 4, 13
 
 
 def tile_multiscaleretention_pa_t_kernel(tc, x, sin, cos, Wq, Wk, out_0, out_1):
@@ -77,7 +78,8 @@ def tile_multiscaleretention_pa_t_kernel(tc, x, sin, cos, Wq, Wk, out_0, out_1):
             )
 
         halves = (slice(0, WIDTH // 2), slice(WIDTH // 2, WIDTH))
-        load_x(0, slice(0, 2))
+        for piece in range(XROWS):
+            load_x(0, slice(2 * piece // XROWS, 2 * (piece + 1) // XROWS))
         load_weight("q", Wq, halves[:1])
         load_table(cos, cos_rows, 0, 1)
         load_table(sin, sin_rows, 0, 1)
@@ -128,8 +130,14 @@ def tile_multiscaleretention_pa_t_kernel(tc, x, sin, cos, Wq, Wk, out_0, out_1):
         w_parts = {}
 
         def lay_out_weight(which, half, copy):
-            w_grouped = weights.tile([P, WIDTH // 2, PACK], BF16, align_bytes=64, tag="w_grouped")
             part = slice(half * WIDTH // 2, (half + 1) * WIDTH // 2)
+            if KWHOLE and which == "k":
+                if half == 0:
+                    whole = weights.tile([P, WIDTH, PACK], BF16, align_bytes=64, tag="whole")
+                    w_parts[which, 0] = whole
+                copy(out=w_parts[which, 0][:, part, :], in_=w_rows[which][:, :, part].rearrange("p t c -> p c t"))
+                return
+            w_grouped = weights.tile([P, WIDTH // 2, PACK], BF16, align_bytes=64, tag="w_grouped")
             copy(out=w_grouped[:], in_=w_rows[which][:, :, part].rearrange("p t c -> p c t"))
             w_parts[which, half] = w_grouped
 
@@ -139,6 +147,8 @@ def tile_multiscaleretention_pa_t_kernel(tc, x, sin, cos, Wq, Wk, out_0, out_1):
                 w_scales = const.tile([P, WIDTH], U8, align_bytes=64, name="w_scales_" + which)
                 w_mx[which] = (w_codes, w_scales)
             part = slice(half * WIDTH // 2, (half + 1) * WIDTH // 2)
+            if KWHOLE and which == "k":
+                part = slice(0, WIDTH)
             nc.vector.quantize_mx(
                 out=w_mx[which][0][:, part].bitcast(FP8X4),
                 scales=w_mx[which][1][:, part],
@@ -172,11 +182,14 @@ def tile_multiscaleretention_pa_t_kernel(tc, x, sin, cos, Wq, Wk, out_0, out_1):
                 words = x_groups[ns[slot]][:, 2 * half + r, :].bitcast(F32)
                 for u in range(2):
                     nc.tensor.transpose(x_t[:, r, u, :], words[:, u : 2 * P : 2], identity[:])
-            first = slot * GROUP + 2 * half * P
-            nc.scalar.copy(
-                out=grouped_words[:, first : first + 2 * P, :].rearrange("p (r m) u -> p r m u", r=2),
-                in_=x_t[:].rearrange("p r u m -> p r m u"),
-            )
+            pieces = XROWS if ns == (0,) and half == 0 else 1
+            for piece in range(pieces):
+                rows = slice(2 * piece // pieces, 2 * (piece + 1) // pieces)
+                first = slot * GROUP + 2 * half * P
+                nc.scalar.copy(
+                    out=grouped_words[:, first + rows.start * P : first + rows.stop * P, :].rearrange("p (r m) u -> p r m u", m=P),
+                    in_=x_t[:, rows].rearrange("p r u m -> p r m u"),
+                )
 
         def quantise_x(ns, pieces=1, piece=0):
             if ns[0] not in x_ops:
@@ -241,6 +254,10 @@ def tile_multiscaleretention_pa_t_kernel(tc, x, sin, cos, Wq, Wk, out_0, out_1):
                         stop=True,
                     )
 
+        def parts_of(i):
+            pieces = 2 if i + TAIL >= len(units) else 1
+            return [slice(t * GROUP // pieces, (t + 1) * GROUP // pieces) for t in range(pieces)]
+
         def rotate(i, cols=slice(0, GROUP)):
             kind, n, b, g, which, h = units[i]
             bank = banks[i]
@@ -288,18 +305,12 @@ def tile_multiscaleretention_pa_t_kernel(tc, x, sin, cos, Wq, Wk, out_0, out_1):
             prod = products.pop(i)
             result = results.tile([P, GROUP], F32, tag="result")
             if kind in "NAG":
-                if i + 1 == len(units) and TAIL > 1:
-                    view = outputs[which][b, h].rearrange("(g p r) c -> g p (r c)", p=P, r=ROWS)[g]
-                    for t in range(TAIL):
-                        part = slice(t * GROUP // TAIL, (t + 1) * GROUP // TAIL)
-                        nc.vector.tensor_tensor(out=result[:, part], in0=prod[:, 0, part], in1=prod[:, 1, part], op=ADD)
-                        nc.sync.dma_start(out=view[:, part], in_=result[:, part])
-                    return
                 adder = nc.vector if i + 1 == len(units) or kind == "A" else nc.gpsimd
-                pieces = 2 if any(0 <= XQ + XSTRIDE * s - i < GSPLIT for s in range(GROUPS_PER_SEQ - 1)) else 1
-                for t in range(pieces):
-                    part = slice(t * GROUP // pieces, (t + 1) * GROUP // pieces)
+                view = outputs[which][b, h].rearrange("(g p r) c -> g p (r c)", p=P, r=ROWS)[g]
+                for part in parts_of(i):
                     adder.tensor_tensor(out=result[:, part], in0=prod[:, 0, part], in1=prod[:, 1, part], op=ADD)
+                    nc.sync.dma_start(out=view[:, part], in_=result[:, part])
+                return
             else:
                 bank = psum_o.tile([P, ROWS, P], F32, tag="o")
                 for r in range(ROWS):
@@ -348,11 +359,11 @@ def tile_multiscaleretention_pa_t_kernel(tc, x, sin, cos, Wq, Wk, out_0, out_1):
             for f in due.pop(i, []):
                 finish(f)
             if i < total:
-                if i + 1 == total:
-                    for t in range(TAIL):
-                        rotate(i, slice(t * GROUP // TAIL, (t + 1) * GROUP // TAIL))
+                if i < EARLY:
+                    rotate(i, early[1])
                 elif not (DEARLY and units[i][0] == "D"):
-                    rotate(i, early[1] if i < EARLY else slice(0, GROUP))
+                    for part in parts_of(i):
+                        rotate(i, part)
                 lag = LAG[units[i][0]]
                 if units[i][0] in "TD":
                     lag += -(i + lag) % PAIRED

@@ -22,7 +22,7 @@ GROUPS_PER_SEQ = SEQ // GROUP
 FLOPS = 2 * BATCH * SEQ * WIDTH * (2 * WIDTH)
 
 PATTERN = "NNNNNNTNDTTNTNNN" + "DTTNNTNNDTTNTNNN" * 3
-KWHOLE = 1
+KWHOLE, KQ = 1, 1
 X1P, DEARLY, TAIL, XROWS = (1, 2), 0, 2, 1
 EARLY, X1Q, TURN, TABLES, QLAY, KLAY = 2, 5, 1, 3, 1, 0
 LEAD, STEP, WARM, PAIRED, SPLIT = 2, 2, 0, 1, 1
@@ -67,13 +67,12 @@ def tile_multiscaleretention_pa_t_kernel(tc, x, sin, cos, Wq, Wk, out_0, out_1):
                 out=x_groups[n][:, part, :], in_=x[b].rearrange("(g p r) c -> g p r c", p=P, r=ROWS)[g][:, part, :]
             )
 
-        cos_rows = const.tile([P, GROUPS_PER_SEQ, GROUP], BF16, name="cos_rows")
+        tables_n = const.tile([P, GROUPS_PER_SEQ, 2, GROUP], BF16, name="tables_n")
         sin_rows = const.tile([P, GROUPS_PER_SEQ, GROUP], BF16, name="sin_rows")
-        sin_turned = const.tile([P, GROUPS_PER_SEQ, GROUP], BF16, name="sin_turned")
 
         def load_table(table, rows, g0, g1):
             nc.sync.dma_start(
-                out=rows[:, g0:g1, :],
+                out=rows,
                 in_=table.rearrange("(g p r) c -> p g (r c)", p=P, r=ROWS)[:, g0:g1, :],
             )
 
@@ -81,14 +80,14 @@ def tile_multiscaleretention_pa_t_kernel(tc, x, sin, cos, Wq, Wk, out_0, out_1):
         for piece in range(XROWS):
             load_x(0, slice(2 * piece // XROWS, 2 * (piece + 1) // XROWS))
         load_weight("q", Wq, halves[:1])
-        load_table(cos, cos_rows, 0, 1)
-        load_table(sin, sin_rows, 0, 1)
+        load_table(cos, tables_n[:, 0:1, 0, :], 0, 1)
+        load_table(sin, sin_rows[:, 0:1, :], 0, 1)
         load_x(0, slice(2, 4))
         load_weight("q", Wq, halves[1:])
         load_weight("k", Wk, (slice(0, WIDTH),))
         load_x(1)
-        load_table(cos, cos_rows, 1, GROUPS_PER_SEQ)
-        load_table(sin, sin_rows, 1, GROUPS_PER_SEQ)
+        load_table(cos, tables_n[:, 1:GROUPS_PER_SEQ, 0, :], 1, GROUPS_PER_SEQ)
+        load_table(sin, sin_rows[:, 1:GROUPS_PER_SEQ, :], 1, GROUPS_PER_SEQ)
         for n in range(2, len(groups)):
             load_x(n)
 
@@ -102,27 +101,19 @@ def tile_multiscaleretention_pa_t_kernel(tc, x, sin, cos, Wq, Wk, out_0, out_1):
         identity_bf = const.tile([P, P], BF16, name="identity_bf")
         nc.gpsimd.tensor_copy(out=identity_bf[:], in_=identity[:])
 
-        def prepare_sin(g, copy, mul):
-            negate_sin(g, mul)
-            turn_sin(g, copy)
-
-        def negate_sin(g, mul):
+        def turn_sin(g):
             pairs = sin_rows[:, g, :].rearrange("p (n e) -> p n e", e=2)
-            mul(out=pairs[:, :, 0], in_=pairs[:, :, 0], mul=-1.0)
-
-        def turn_sin(g, copy):
-            pairs = sin_rows[:, g, :].rearrange("p (n e) -> p n e", e=2)
-            turned = sin_turned[:, g, :].rearrange("p (n e) -> p n e", e=2)
-            copy(out=turned[:, :, 1], in_=pairs[:, :, 0])
-            copy(out=turned[:, :, 0], in_=pairs[:, :, 1])
+            turned = tables_n[:, g, 1, :].rearrange("p (n e) -> p n e", e=2)
+            nc.scalar.copy(out=turned[:, :, 0], in_=pairs[:, :, 1])
+            nc.scalar.mul(out=turned[:, :, 1], in_=pairs[:, :, 0], mul=-1.0)
 
         tables_t = const.tile([P, GROUPS_PER_SEQ, 2, GROUP], BF16, name="tables_t")
 
         def transpose_tables(g):
             bank = psum_o.tile([P, 2, ROWS, P], BF16, tag="o")
-            for v, rows in enumerate((cos_rows, sin_turned)):
+            for v in range(2):
                 for r in range(ROWS):
-                    nc.tensor.transpose(bank[:, v, r, :], rows[:, g, r * P : (r + 1) * P], identity_bf[:])
+                    nc.tensor.transpose(bank[:, v, r, :], tables_n[:, g, v, r * P : (r + 1) * P], identity_bf[:])
             nc.scalar.copy(out=tables_t[:, g, :, :].rearrange("p v n -> p (v n)"), in_=bank[:].rearrange("p v r m -> p (v r m)"))
 
         w_mx = {}
@@ -228,8 +219,6 @@ def tile_multiscaleretention_pa_t_kernel(tc, x, sin, cos, Wq, Wk, out_0, out_1):
                 banks[i] = bank
             bank = banks[i]
             for part in parts:
-                if part == 0 and WARM:
-                    nc.tensor.matmul(bank[:, 0:WARM], identity_bf[:], cos_rows[:, 0, 0:WARM], start=True, stop=True)
                 if kind in "NAG":
                     for r in (2 * part, 2 * part + 1):
                         rows = slice(first + r * P, first + (r + 1) * P)
@@ -267,25 +256,13 @@ def tile_multiscaleretention_pa_t_kernel(tc, x, sin, cos, Wq, Wk, out_0, out_1):
                 else:
                     products[i] = work.tile([P, 2, GROUP], F32, tag="prod", name="prod")
             prod = products[i]
-            if kind == "G":
-                u = slow.tile([P, GROUP], F32, tag="u_sb")
-                nc.scalar.mul(out=u[:, cols], in_=bank[:, cols], mul=factor[which])
-                nc.gpsimd.tensor_tensor(out=prod[:, 0, cols], in0=u[:, cols], in1=cos_rows[:, g, cols], op=MULT)
-                nc.gpsimd.tensor_tensor(
-                    out=prod[:, 1, cols].rearrange("p (n e) -> p n e", e=2),
-                    in0=u[:, cols].rearrange("p (n e) -> p n e", e=2)[:, :, ::-1],
-                    in1=sin_rows[:, g, cols].rearrange("p (n e) -> p n e", e=2),
-                    op=MULT,
-                )
-            elif kind in "NA":
+            if kind in "NA":
+                width = cols.stop - cols.start
                 nc.vector.scalar_tensor_tensor(
-                    out=prod[:, 0, cols], in0=bank[:, cols], scalar=factor[which], in1=cos_rows[:, g, cols], op0=MULT, op1=MULT
-                )
-                nc.vector.scalar_tensor_tensor(
-                    out=prod[:, 1, cols].rearrange("p (n e) -> p n e", e=2),
-                    in0=bank[:, cols].rearrange("p (n e) -> p n e", e=2)[:, :, ::-1],
+                    out=prod[:, :, cols],
+                    in0=bank[:, cols].unsqueeze(1).to_broadcast([P, 2, width]),
                     scalar=factor[which],
-                    in1=sin_rows[:, g, cols].rearrange("p (n e) -> p n e", e=2),
+                    in1=tables_n[:, g, :, cols],
                     op0=MULT,
                     op1=MULT,
                 )
@@ -308,7 +285,12 @@ def tile_multiscaleretention_pa_t_kernel(tc, x, sin, cos, Wq, Wk, out_0, out_1):
                 adder = nc.vector if i + 1 == len(units) or kind == "A" else nc.gpsimd
                 view = outputs[which][b, h].rearrange("(g p r) c -> g p (r c)", p=P, r=ROWS)[g]
                 for part in parts_of(i):
-                    adder.tensor_tensor(out=result[:, part], in0=prod[:, 0, part], in1=prod[:, 1, part], op=ADD)
+                    adder.tensor_tensor(
+                        out=result[:, part].rearrange("p (n e) -> p n e", e=2),
+                        in0=prod[:, 0, part].rearrange("p (n e) -> p n e", e=2),
+                        in1=prod[:, 1, part].rearrange("p (n e) -> p n e", e=2)[:, :, ::-1],
+                        op=ADD,
+                    )
                     nc.sync.dma_start(out=view[:, part], in_=result[:, part])
                 return
             else:
@@ -326,7 +308,7 @@ def tile_multiscaleretention_pa_t_kernel(tc, x, sin, cos, Wq, Wk, out_0, out_1):
         transpose_x((0,), 0, 0)
         lay_out_weight("q", 0, nc.vector.tensor_copy)
         quantise_x((0,), 2, 0)
-        negate_sin(0, nc.scalar.mul)
+        turn_sin(0)
         transpose_x((0,), 0, 1)
         if QLAY == 0:
             lay_out_weight("q", 1, nc.scalar.copy)
@@ -341,8 +323,6 @@ def tile_multiscaleretention_pa_t_kernel(tc, x, sin, cos, Wq, Wk, out_0, out_1):
             multiply(i, (1,))
         for i in range(EARLY, LEAD):
             multiply(i)
-        if TURN < 0:
-            turn_sin(0, nc.scalar.copy)
         lay_out_weight("k", 0, nc.scalar.copy if KLAY == 0 else nc.vector.tensor_copy)
         if KLAY < 2:
             lay_out_weight("k", 1, nc.scalar.copy)
@@ -356,6 +336,8 @@ def tile_multiscaleretention_pa_t_kernel(tc, x, sin, cos, Wq, Wk, out_0, out_1):
                     multiply(m)
                     if DEARLY and units[m][0] == "D":
                         rotate(m)
+            if i == KQ and ("k", 0) in w_parts:
+                quantise_weight("k", 0)
             for f in due.pop(i, []):
                 finish(f)
             if i < total:
@@ -373,8 +355,6 @@ def tile_multiscaleretention_pa_t_kernel(tc, x, sin, cos, Wq, Wk, out_0, out_1):
                     lay_out_weight("k", 1, nc.vector.tensor_copy)
                 if phase in X1P:
                     transpose_x((1,), 0, X1P.index(phase))
-                if phase == TURN:
-                    turn_sin(0, nc.scalar.copy)
                 if phase == TABLES:
                     transpose_tables(0)
                 if phase == X1Q:
@@ -391,6 +371,6 @@ def tile_multiscaleretention_pa_t_kernel(tc, x, sin, cos, Wq, Wk, out_0, out_1):
                 if place == XQ:
                     quantise_x(ns)
                 if place == SINP:
-                    prepare_sin(pair, nc.scalar.copy, nc.scalar.mul)
+                    turn_sin(pair)
                 if place == TB:
                     transpose_tables(pair)

@@ -23,6 +23,7 @@ FLOPS = 2 * BATCH * SEQ * WIDTH * (2 * WIDTH)
 
 PATTERN = "NNNNNNTNDTTNTNNN" + "DTTNNTNNDTTNTNNN" * 3
 KWHOLE, KQ = 1, 1
+NSHARE, NBUFS, TBUFS = 4, 3, 3
 X1P, DEARLY, TAIL, XROWS = (1, 2), 0, 2, 1
 EARLY, X1Q, TURN, TABLES, QLAY, KLAY = 2, 5, 1, 3, 1, 0
 LEAD, STEP, WARM, PAIRED, SPLIT = 2, 2, 0, 1, 1
@@ -42,7 +43,7 @@ def tile_multiscaleretention_pa_t_kernel(tc, x, sin, cos, Wq, Wk, out_0, out_1):
         x_mx = stack.enter_context(tc.tile_pool(name="x_mx", bufs=2))
         work = stack.enter_context(tc.tile_pool(name="work", bufs=10))
         slow = stack.enter_context(tc.tile_pool(name="slow", bufs=3))
-        results = stack.enter_context(tc.tile_pool(name="results", bufs=10))
+        results = stack.enter_context(tc.tile_pool(name="results", bufs=8))
         psum_x = stack.enter_context(tc.psum_pool(name="psum_x", bufs=1))
         psum_u = stack.enter_context(tc.psum_pool(name="psum_u", bufs=5))
         psum_o = stack.enter_context(tc.psum_pool(name="psum_o", bufs=2))
@@ -206,6 +207,8 @@ def tile_multiscaleretention_pa_t_kernel(tc, x, sin, cos, Wq, Wk, out_0, out_1):
                     units.append((PATTERN[len(units)], n, b, g, which, h))
         banks = {}
         products = {}
+        n_units = [i for i, unit in enumerate(units) if unit[0] == "N"]
+        n_tiles = []
 
         def multiply(i, parts=(0, 1)):
             kind, n, b, g, which, h = units[i]
@@ -251,10 +254,16 @@ def tile_multiscaleretention_pa_t_kernel(tc, x, sin, cos, Wq, Wk, out_0, out_1):
             kind, n, b, g, which, h = units[i]
             bank = banks[i]
             if i not in products:
-                if kind in "DG":
+                if kind == "D":
                     products[i] = slow.tile([P, 2, GROUP], F32, tag="prod_d", name="prod_d")
+                elif kind == "T":
+                    products[i] = work.tile([P, 2, GROUP], F32, tag="prod_t", name="prod_t", bufs=TBUFS)
                 else:
-                    products[i] = work.tile([P, 2, GROUP], F32, tag="prod", name="prod")
+                    order = n_units.index(i)
+                    if order % NSHARE == 0:
+                        shared = work.tile([P, NSHARE, 2, GROUP], F32, tag="prod_n", name="prod_n", bufs=NBUFS)
+                        n_tiles.append(shared)
+                    products[i] = n_tiles[-1][:, order % NSHARE, :, :]
             prod = products[i]
             if kind in "NA":
                 width = cols.stop - cols.start

from contextlib import ExitStack

import concourse.mybir as mybir
from concourse.masks import make_identity

F32 = mybir.dt.float32
BF16 = mybir.dt.bfloat16
U32 = mybir.dt.uint32
U8 = mybir.dt.uint8
FP8X4 = mybir.dt.float8_e4m3fn_x4
MULT = mybir.AluOpType.mult
ADD = mybir.AluOpType.add

P = 128
PACK = 4
BATCH, SEQ, WIDTH = 2, 2048, 512
HEADS, HEAD_DIM = 4, 128
ROWS = 4
GROUP = P * ROWS
GROUPS_PER_SEQ = SEQ // GROUP

FLOPS = 2 * BATCH * SEQ * WIDTH * (2 * WIDTH)

PATTERN = "NNNNNNTNDTTNTNNN" + "DTTNNTNNDTTNTNNN" * 3
KWHOLE, KQ = 1, 1
NSHARE, NBUFS, TBUFS = 4, 3, 3
X1P, DEARLY, TAIL, XROWS = (1, 2), 0, 2, 1
EARLY, X1Q, TURN, TABLES, QLAY, KLAY = 2, 5, 1, 3, 1, 0
LEAD, STEP, WARM, PAIRED, SPLIT = 2, 2, 0, 1, 1
LAG = {"A": 1, "G": 1, "N": 1, "T": 1, "D": 6}
XSTART, XSTRIDE = 0, 16
XPLACES, XQ, SINP, TB = (4, 6, 8, 10), 13, 4, 13


def tile_multiscaleretention_pa_t_kernel(tc, x, sin, cos, Wq, Wk, out_0, out_1):
    nc = tc.nc
    groups = [(b, g) for g in range(GROUPS_PER_SEQ) for b in range(BATCH)]
    with ExitStack() as stack:
        stack.enter_context(tc.manual_schedule())
        const = stack.enter_context(tc.tile_pool(name="const", bufs=1))
        weights = stack.enter_context(tc.tile_pool(name="weights", bufs=4))
        x_pool = stack.enter_context(tc.tile_pool(name="x_rows", bufs=len(groups)))
        x_mx = stack.enter_context(tc.tile_pool(name="x_mx", bufs=2))
        work = stack.enter_context(tc.tile_pool(name="work", bufs=10))
        slow = stack.enter_context(tc.tile_pool(name="slow", bufs=3))
        results = stack.enter_context(tc.tile_pool(name="results", bufs=8))
        psum_x = stack.enter_context(tc.psum_pool(name="psum_x", bufs=1))
        psum_u = stack.enter_context(tc.psum_pool(name="psum_u", bufs=5))
        psum_o = stack.enter_context(tc.psum_pool(name="psum_o", bufs=2))

        w_rows = {}

        def load_weight(which, w, pieces):
            if which not in w_rows:
                rows = const.tile([P, PACK, WIDTH], BF16, name="w_rows_" + which)
                w_rows[which] = rows
            for part in pieces:
                nc.sync.dma_start(out=w_rows[which][:, :, part], in_=w.rearrange("(p t) c -> p t c", t=PACK)[:, :, part])

        x_groups = {}

        def load_x(n, part=slice(0, ROWS)):
            b, g = groups[n]
            if n not in x_groups:
                x_rows = x_pool.tile([P, ROWS, WIDTH], BF16)
                x_groups[n] = x_rows
            nc.sync.dma_start(
                out=x_groups[n][:, part, :], in_=x[b].rearrange("(g p r) c -> g p r c", p=P, r=ROWS)[g][:, part, :]
            )

        tables_n = const.tile([P, GROUPS_PER_SEQ, 2, GROUP], BF16, name="tables_n")
        sin_rows = const.tile([P, GROUPS_PER_SEQ, GROUP], BF16, name="sin_rows")

        def load_table(table, rows, g0, g1):
            nc.sync.dma_start(
                out=rows,
                in_=table.rearrange("(g p r) c -> p g (r c)", p=P, r=ROWS)[:, g0:g1, :],
            )

        halves = (slice(0, WIDTH // 2), slice(WIDTH // 2, WIDTH))
        for piece in range(XROWS):
            load_x(0, slice(2 * piece // XROWS, 2 * (piece + 1) // XROWS))
        load_weight("q", Wq, halves[:1])
        load_table(cos, tables_n[:, 0:1, 0, :], 0, 1)
        load_table(sin, sin_rows[:, 0:1, :], 0, 1)
        load_x(0, slice(2, 4))
        load_weight("q", Wq, halves[1:])
        load_weight("k", Wk, (slice(0, WIDTH),))
        load_x(1)
        load_table(cos, tables_n[:, 1:GROUPS_PER_SEQ, 0, :], 1, GROUPS_PER_SEQ)
        load_table(sin, sin_rows[:, 1:GROUPS_PER_SEQ, :], 1, GROUPS_PER_SEQ)
        for n in range(2, len(groups)):
            load_x(n)

        identity = const.tile([P, P], F32, name="identity")
        make_identity(nc, identity[:])
        swap = const.tile([P, P], F32, name="swap")
        identity_pairs = identity[:].rearrange("p (n e) -> p n e", e=2)
        swap_pairs = swap[:].rearrange("p (n e) -> p n e", e=2)
        for e in range(2):
            nc.gpsimd.tensor_copy(out=swap_pairs[:, :, e], in_=identity_pairs[:, :, 1 - e])
        identity_bf = const.tile([P, P], BF16, name="identity_bf")
        nc.gpsimd.tensor_copy(out=identity_bf[:], in_=identity[:])

        def turn_sin(g):
            pairs = sin_rows[:, g, :].rearrange("p (n e) -> p n e", e=2)
            turned = tables_n[:, g, 1, :].rearrange("p (n e) -> p n e", e=2)
            nc.scalar.copy(out=turned[:, :, 0], in_=pairs[:, :, 1])
            nc.scalar.mul(out=turned[:, :, 1], in_=pairs[:, :, 0], mul=-1.0)

        tables_t = const.tile([P, GROUPS_PER_SEQ, 2, GROUP], BF16, name="tables_t")

        def transpose_tables(g):
            bank = psum_o.tile([P, 2, ROWS, P], BF16, tag="o")
            for v in range(2):
                for r in range(ROWS):
                    nc.tensor.transpose(bank[:, v, r, :], tables_n[:, g, v, r * P : (r + 1) * P], identity_bf[:])
            nc.scalar.copy(out=tables_t[:, g, :, :].rearrange("p v n -> p (v n)"), in_=bank[:].rearrange("p v r m -> p (v r m)"))

        w_mx = {}

        w_parts = {}

        def lay_out_weight(which, half, copy):
            part = slice(half * WIDTH // 2, (half + 1) * WIDTH // 2)
            if KWHOLE and which == "k":
                if half == 0:
                    whole = weights.tile([P, WIDTH, PACK], BF16, align_bytes=64, tag="whole")
                    w_parts[which, 0] = whole
                copy(out=w_parts[which, 0][:, part, :], in_=w_rows[which][:, :, part].rearrange("p t c -> p c t"))
                return
            w_grouped = weights.tile([P, WIDTH // 2, PACK], BF16, align_bytes=64, tag="w_grouped")
            copy(out=w_grouped[:], in_=w_rows[which][:, :, part].rearrange("p t c -> p c t"))
            w_parts[which, half] = w_grouped

        def quantise_weight(which, half):
            if which not in w_mx:
                w_codes = const.tile([P, WIDTH], U32, align_bytes=64, name="w_codes_" + which)
                w_scales = const.tile([P, WIDTH], U8, align_bytes=64, name="w_scales_" + which)
                w_mx[which] = (w_codes, w_scales)
            part = slice(half * WIDTH // 2, (half + 1) * WIDTH // 2)
            if KWHOLE and which == "k":
                part = slice(0, WIDTH)
            nc.vector.quantize_mx(
                out=w_mx[which][0][:, part].bitcast(FP8X4),
                scales=w_mx[which][1][:, part],
                in_=w_parts.pop((which, half))[:].rearrange("p c t -> p (c t)"),
            )

        x_laid = {}
        x_ops = {}

        x_split = {}

        def split_x(n):
            split = x_mx.tile([P, ROWS, 2, P], F32, tag="split", bufs=3)
            nc.scalar.copy(
                out=split[:], in_=x_groups[n][:].bitcast(F32).rearrange("p r (m u) -> p r u m", u=2)
            )
            x_split[n] = split

        def transpose_x(ns, slot, half):
            if ns not in x_laid:
                x_grouped = x_mx.tile([P, len(ns) * GROUP, PACK], BF16, align_bytes=64, tag="grouped%d" % len(ns))
                x_laid[ns] = x_grouped
            grouped_words = x_laid[ns][:].bitcast(F32)
            x_t = psum_x.tile([P, 2, 2, P], F32)
            for r in range(2):
                if ns[slot] in x_split:
                    words = x_split[ns[slot]][:, 2 * half + r, :, :]
                    for u in range(2):
                        nc.tensor.transpose(x_t[:, r, u, :], words[:, u, :], identity[:])
                    continue
                words = x_groups[ns[slot]][:, 2 * half + r, :].bitcast(F32)
                for u in range(2):
                    nc.tensor.transpose(x_t[:, r, u, :], words[:, u : 2 * P : 2], identity[:])
            pieces = XROWS if ns == (0,) and half == 0 else 1
            for piece in range(pieces):
                rows = slice(2 * piece // pieces, 2 * (piece + 1) // pieces)
                first = slot * GROUP + 2 * half * P
                nc.scalar.copy(
                    out=grouped_words[:, first + rows.start * P : first + rows.stop * P, :].rearrange("p (r m) u -> p r m u", m=P),
                    in_=x_t[:, rows].rearrange("p r u m -> p r m u"),
                )

        def quantise_x(ns, pieces=1, piece=0):
            if ns[0] not in x_ops:
                x_codes = x_mx.tile([P, len(ns) * GROUP], U32, align_bytes=64, tag="codes%d" % len(ns))
                x_scales = x_mx.tile([P, len(ns) * GROUP], U8, align_bytes=64, tag="scales%d" % len(ns))
                for slot, n in enumerate(ns):
                    x_ops[n] = (x_codes, x_scales, slot * GROUP)
            width = len(ns) * GROUP // pieces
            part = slice(piece * width, (piece + 1) * width)
            nc.vector.quantize_mx(
                out=x_ops[ns[0]][0][:, part].bitcast(FP8X4),
                scales=x_ops[ns[0]][1][:, part],
                in_=x_laid[ns][:, part, :].rearrange("p m t -> p (m t)"),
            )

        factor = {"q": 1.0, "k": HEAD_DIM**-0.5}
        outputs = {"q": out_0, "k": out_1}

        units = []
        for n, (b, g) in enumerate(groups):
            for which in ("q", "k"):
                for h in range(HEADS):
                    units.append((PATTERN[len(units)], n, b, g, which, h))
        banks = {}
        products = {}
        n_units = [i for i, unit in enumerate(units) if unit[0] == "N"]
        n_tiles = []

        def multiply(i, parts=(0, 1)):
            kind, n, b, g, which, h = units[i]
            if (which, h * 2 // HEADS) in w_parts:
                quantise_weight(which, h * 2 // HEADS)
            w_codes, w_scales = w_mx[which]
            x_codes, x_scales, first = x_ops[n]
            cols = slice(h * HEAD_DIM, (h + 1) * HEAD_DIM)
            if i not in banks:
                bank = psum_u.tile([P, GROUP], F32, tag="u")
                banks[i] = bank
            bank = banks[i]
            for part in parts:
                if kind in "NAG":
                    for r in (2 * part, 2 * part + 1):
                        rows = slice(first + r * P, first + (r + 1) * P)
                        nc.tensor.matmul_mx(
                            out=bank[:, r * P : (r + 1) * P],
                            lhsT=x_codes[:, rows].bitcast(FP8X4),
                            lhsT_scale=x_scales[:, rows],
                            rhs=w_codes[:, cols].bitcast(FP8X4),
                            rhs_scale=w_scales[:, cols],
                            start=True,
                            stop=True,
                        )
                else:
                    rows = slice(first + part * 2 * P, first + (part + 1) * 2 * P)
                    nc.tensor.matmul_mx(
                        out=bank[:, part * 2 * P : (part + 1) * 2 * P],
                        lhsT=w_codes[:, cols].bitcast(FP8X4),
                        lhsT_scale=w_scales[:, cols],
                        rhs=x_codes[:, rows].bitcast(FP8X4),
                        rhs_scale=x_scales[:, rows],
                        start=True,
                        stop=True,
                    )

        def parts_of(i):
            pieces = 2 if i + TAIL >= len(units) else 1
            return [slice(t * GROUP // pieces, (t + 1) * GROUP // pieces) for t in range(pieces)]

        def rotate(i, cols=slice(0, GROUP)):
            kind, n, b, g, which, h = units[i]
            bank = banks[i]
            if i not in products:
                if kind == "D":
                    products[i] = slow.tile([P, 2, GROUP], F32, tag="prod_d", name="prod_d")
                elif kind == "T":
                    products[i] = work.tile([P, 2, GROUP], F32, tag="prod_t", name="prod_t", bufs=TBUFS)
                else:
                    order = n_units.index(i)
                    if order % NSHARE == 0:
                        shared = work.tile([P, NSHARE, 2, GROUP], F32, tag="prod_n", name="prod_n", bufs=NBUFS)
                        n_tiles.append(shared)
                    products[i] = n_tiles[-1][:, order % NSHARE, :, :]
            prod = products[i]
            if kind in "NA":
                width = cols.stop - cols.start
                nc.vector.scalar_tensor_tensor(
                    out=prod[:, :, cols],
                    in0=bank[:, cols].unsqueeze(1).to_broadcast([P, 2, width]),
                    scalar=factor[which],
                    in1=tables_n[:, g, :, cols],
                    op0=MULT,
                    op1=MULT,
                )
            elif kind == "T":
                nc.vector.tensor_tensor(
                    out=prod[:], in0=bank[:].unsqueeze(1).to_broadcast([P, 2, GROUP]), in1=tables_t[:, g, :, :], op=MULT
                )
            else:
                u = slow.tile([P, GROUP], F32, tag="u_sb")
                nc.scalar.copy(out=u[:], in_=bank[:])
                nc.gpsimd.tensor_tensor(
                    out=prod[:], in0=u[:].unsqueeze(1).to_broadcast([P, 2, GROUP]), in1=tables_t[:, g, :, :], op=MULT
                )

        def finish(i):
            kind, n, b, g, which, h = units[i]
            prod = products.pop(i)
            result = results.tile([P, GROUP], F32, tag="result")
            if kind in "NAG":
                adder = nc.vector if i + 1 == len(units) or kind == "A" else nc.gpsimd
                view = outputs[which][b, h].rearrange("(g p r) c -> g p (r c)", p=P, r=ROWS)[g]
                for part in parts_of(i):
                    adder.tensor_tensor(
                        out=result[:, part].rearrange("p (n e) -> p n e", e=2),
                        in0=prod[:, 0, part].rearrange("p (n e) -> p n e", e=2),
                        in1=prod[:, 1, part].rearrange("p (n e) -> p n e", e=2)[:, :, ::-1],
                        op=ADD,
                    )
                    nc.sync.dma_start(out=view[:, part], in_=result[:, part])
                return
            else:
                bank = psum_o.tile([P, ROWS, P], F32, tag="o")
                for r in range(ROWS):
                    part = slice(r * P, (r + 1) * P)
                    nc.tensor.matmul(bank[:, r, :], prod[:, 0, part], identity[:], start=True, stop=False, is_transpose=True)
                    nc.tensor.matmul(bank[:, r, :], prod[:, 1, part], swap[:], start=False, stop=True, is_transpose=True)
                nc.scalar.mul(out=result[:], in_=bank[:].rearrange("p r c -> p (r c)"), mul=factor[which])
            nc.sync.dma_start(
                out=outputs[which][b, h].rearrange("(g p r) c -> g p (r c)", p=P, r=ROWS)[g], in_=result[:]
            )

        early = (slice(0, GROUP // 2), slice(GROUP // 2, GROUP))
        transpose_x((0,), 0, 0)
        lay_out_weight("q", 0, nc.vector.tensor_copy)
        quantise_x((0,), 2, 0)
        turn_sin(0)
        transpose_x((0,), 0, 1)
        if QLAY == 0:
            lay_out_weight("q", 1, nc.scalar.copy)
        for i in range(EARLY):
            multiply(i, (0,))
        if QLAY == 1:
            lay_out_weight("q", 1, nc.vector.tensor_copy)
        for i in range(EARLY):
            rotate(i, early[0])
        quantise_x((0,), 2, 1)
        for i in range(EARLY):
            multiply(i, (1,))
        for i in range(EARLY, LEAD):
            multiply(i)
        lay_out_weight("k", 0, nc.scalar.copy if KLAY == 0 else nc.vector.tensor_copy)
        if KLAY < 2:
            lay_out_weight("k", 1, nc.scalar.copy)
        total = len(units)
        per_group = 2 * HEADS
        due = {}
        for i in range(total + max(LAG.values()) + 2):
            n, phase = divmod(i, per_group)
            if i % STEP == 0:
                for m in range(i + LEAD, min(i + LEAD + STEP, total)):
                    multiply(m)
                    if DEARLY and units[m][0] == "D":
                        rotate(m)
            if i == KQ and ("k", 0) in w_parts:
                quantise_weight("k", 0)
            for f in due.pop(i, []):
                finish(f)
            if i < total:
                if i < EARLY:
                    rotate(i, early[1])
                elif not (DEARLY and units[i][0] == "D"):
                    for part in parts_of(i):
                        rotate(i, part)
                lag = LAG[units[i][0]]
                if units[i][0] in "TD":
                    lag += -(i + lag) % PAIRED
                due.setdefault(i + lag, []).append(i)
            if n == 0:
                if phase == 1 and KLAY == 2:
                    lay_out_weight("k", 1, nc.vector.tensor_copy)
                if phase in X1P:
                    transpose_x((1,), 0, X1P.index(phase))
                if phase == TABLES:
                    transpose_tables(0)
                if phase == X1Q:
                    quantise_x((1,))
            for pair in range(1, GROUPS_PER_SEQ):
                ns = (BATCH * pair, BATCH * pair + 1)
                place = i - XSTART - XSTRIDE * (pair - 1)
                if SPLIT and place in (0, 1):
                    split_x(ns[place])
                if place in XPLACES:
                    for k in range(4):
                        if XPLACES[k] == place:
                            transpose_x(ns, k // 2, k % 2)
                if place == XQ:
                    quantise_x(ns)
                if place == SINP:
                    turn_sin(pair)
                if place == TB:
                    transpose_tables(pair)
